import numpy as np
import ml_dtypes


def mxq(x, axis, fmt="e4m3"):
    dtype, down = {"e4m3": (ml_dtypes.float8_e4m3fn, 7), "e5m2": (ml_dtypes.float8_e5m2, 14)}[fmt]
    v = np.moveaxis(np.asarray(x, np.float32).astype(ml_dtypes.bfloat16).astype(np.float64), axis, -1)
    blocks = v.reshape(v.shape[:-1] + (-1, 32))
    amax = np.abs(blocks).max(-1, keepdims=True)
    byte = np.maximum(np.where(amax > 0, np.frexp(amax)[1] - 1 + 127, 0) - down, 1)
    scale = np.exp2(byte - 127.0)
    codes = (blocks / scale).astype(np.float32).astype(dtype).astype(np.float64)
    return np.moveaxis((codes * scale).reshape(v.shape), -1, axis)


WIDE = False


def mx_kscale(k):
    if not WIDE:
        return np.ones(k)
    levels = np.array([20, 10, 0, 15, 5])
    a = np.random.permutation(np.resize(levels, k // 512 * 4)).reshape(k // 512, 4)
    idx = np.arange(k)
    return np.exp2(a[idx // 512, idx % 128 // 32])


BF16 = ml_dtypes.bfloat16


def bf(x):
    return np.asarray(x, np.float32).astype(BF16)


def f64(x):
    return np.asarray(x).astype(np.float64)


B, IN, OUT, GRID_SIZE, SPLINE_ORDER = 2048, 512, 512, 5, 3
N_COEFF = GRID_SIZE + SPLINE_ORDER


def setup_inputs():
    u = mx_kscale(OUT)
    h = 2.0 / GRID_SIZE
    grid_1d = np.arange(-SPLINE_ORDER, GRID_SIZE + SPLINE_ORDER + 1) * h - 1.0
    grid = grid_1d[None, :] + np.random.uniform(-0.05, 0.05, (IN, grid_1d.shape[0]))
    x = np.random.uniform(-1.0, 1.0, (B, IN))
    base_weight = np.random.uniform(-1.0, 1.0, (OUT, IN)) * 3.0 / np.sqrt(IN) * u[:, None]
    spline_weight = np.random.randint(-5, 6, (OUT, IN, N_COEFF)) / 32.0 * u[:, None, None]
    g = np.random.standard_normal((B, OUT)) * np.exp2(np.random.randint(-12, 1, (B, 1))) / u
    return {"x": bf(x), "base_weight": bf(base_weight), "spline_weight": bf(spline_weight),
            "grid": bf(grid), "grad_out": bf(g)}


def b_splines_and_slopes(x, grid, k):
    xe = x[:, :, None]
    g = grid[None, :, :]
    bases = ((xe >= g[:, :, :-1]) & (xe < g[:, :, 1:])).astype(np.float64)
    slopes = np.zeros_like(bases)
    for p in range(1, k + 1):
        t_i = g[:, :, : -1 - p]
        t_i_p = g[:, :, p:-1]
        d1 = t_i_p - t_i + 1e-8
        t_i_1 = g[:, :, 1:-p]
        t_i_p_1 = g[:, :, p + 1:]
        d2 = t_i_p_1 - t_i_1 + 1e-8
        new_slopes = (bases[:, :, :-1] + (xe - t_i) * slopes[:, :, :-1]) / d1 + ((t_i_p_1 - xe) * slopes[:, :, 1:] - bases[:, :, 1:]) / d2
        bases = (xe - t_i) / d1 * bases[:, :, :-1] + (t_i_p_1 - xe) / d2 * bases[:, :, 1:]
        slopes = new_slopes
    return bases, slopes


def reference(x, base_weight, spline_weight, grid, grad_out):
    gq = mxq(f64(grad_out), 1, "e5m2")
    base_part = gq @ mxq(f64(base_weight), 0, "e4m3")
    coeff = gq @ mxq(f64(spline_weight).reshape(OUT, IN * N_COEFF), 0, "e4m3")
    slopes = b_splines_and_slopes(f64(x), f64(grid), SPLINE_ORDER)[1]
    return base_part + (slopes * coeff.reshape(B, IN, N_COEFF)).sum(axis=2)

@@ -1,0 +1,285 @@
+from contextlib import ExitStack
+
+import concourse.mybir as mybir
+from concourse.masks import make_identity
+
+F32 = mybir.dt.float32
+BF16 = mybir.dt.bfloat16
+U32 = mybir.dt.uint32
+U8 = mybir.dt.uint8
+E4M3X4 = mybir.dt.float8_e4m3fn_x4
+E5M2X4 = mybir.dt.float8_e5m2_x4
+ALU = mybir.AluOpType
+ACT = mybir.ActivationFunctionType
+
+P = 128
+PACK = 4
+B = 2048
+IN = 512
+OUT = 512
+N_C = 8
+N_KNOTS = 12
+N_PIECE = 4
+EPS = 1e-8
+N_IB = IN // P
+N_TB = B // P
+CHUNK = 512
+N_CHUNK = B // CHUNK
+TB_PER_BANK = CHUNK // P
+
+FLOPS = 2 * B * OUT * IN * (N_C + 1)
+
+PATHS = (
+    (1.0, ((0, 0, 0, (0, 0, 0)),)),
+    (-1.0, ((0, 0, 1, (0, 0, 2)), (0, 1, 1, (0, 3, 1)), (1, 1, 1, (4, 1, 1)))),
+    (1.0, ((0, 1, 2, (0, 3, 3)), (1, 1, 2, (4, 1, 3)), (1, 2, 2, (4, 4, 2)))),
+    (-1.0, ((1, 2, 3, (4, 4, 4)),)),
+)
+
+
+def spline_tables(nc, tabs, tmp, kn):
+    vec = nc.vector
+
+    def knot(e):
+        return kn[:, :, e : e + N_C]
+
+    def new(name):
+        return tmp.tile([P, N_IB, N_C], F32, name=name)
+
+    inv_span = {}
+    for s in (1, 2, 3):
+        n = N_KNOTS - s
+        inv = tabs.tile([P, N_IB, n], F32, name="inv_span%d" % s)
+        vec.tensor_sub(out=inv[:], in0=kn[:, :, s:N_KNOTS], in1=kn[:, :, 0:n])
+        vec.tensor_scalar_add(out=inv[:], in0=inv[:], scalar1=EPS)
+        vec.reciprocal(out=inv[:], in_=inv[:])
+        inv_span[s] = inv
+
+    rel = []
+    for e in range(5):
+        r = tabs.tile([P, N_IB, N_C], F32, name="rel%d" % e)
+        vec.tensor_sub(out=r[:], in0=knot(e), in1=knot(2))
+        rel.append(r)
+
+    gain = tabs.tile([P, N_PIECE, N_IB, N_C], F32, name="gain")
+    lin = tabs.tile([P, N_PIECE, N_IB, N_C], F32, name="lin")
+    con = tabs.tile([P, N_PIECE, N_IB, N_C], F32, name="con")
+    bias = tabs.tile([P, N_PIECE, N_IB, N_C], F32, name="bias")
+    lo = tabs.tile([P, N_PIECE, N_IB, N_C], F32, name="lo")
+    hi = tabs.tile([P, N_PIECE, N_IB, N_C], F32, name="hi")
+    offset = tabs.tile([P, N_IB, N_C], F32, name="offset")
+
+    for d in range(N_PIECE):
+        sign, paths = PATHS[d]
+        for n, (e3, e2, e1, (a, b, c)) in enumerate(paths):
+            k = new("k")
+            vec.tensor_mul(out=k[:], in0=inv_span[3][:, :, e3 : e3 + N_C], in1=inv_span[2][:, :, e2 : e2 + N_C])
+            vec.tensor_mul(out=k[:], in0=k[:], in1=inv_span[1][:, :, e1 : e1 + N_C])
+            pair = new("pair")
+            vec.tensor_add(out=pair[:], in0=rel[a][:], in1=rel[b][:])
+            sum1 = new("sum1")
+            vec.tensor_add(out=sum1[:], in0=pair[:], in1=rel[c][:])
+            sum2 = new("sum2")
+            vec.tensor_mul(out=sum2[:], in0=rel[a][:], in1=rel[b][:])
+            cross = new("cross")
+            vec.tensor_mul(out=cross[:], in0=pair[:], in1=rel[c][:])
+            vec.tensor_add(out=sum2[:], in0=sum2[:], in1=cross[:])
+            if n == 0:
+                vec.tensor_copy(out=gain[:, d], in_=k[:])
+                vec.tensor_mul(out=lin[:, d], in0=k[:], in1=sum1[:])
+                vec.tensor_mul(out=con[:, d], in0=k[:], in1=sum2[:])
+            else:
+                vec.tensor_add(out=gain[:, d], in0=gain[:, d], in1=k[:])
+                vec.tensor_mul(out=sum1[:], in0=k[:], in1=sum1[:])
+                vec.tensor_add(out=lin[:, d], in0=lin[:, d], in1=sum1[:])
+                vec.tensor_mul(out=sum2[:], in0=k[:], in1=sum2[:])
+                vec.tensor_add(out=con[:, d], in0=con[:, d], in1=sum2[:])
+        vec.tensor_scalar_mul(out=gain[:, d], in0=gain[:, d], scalar1=3.0 * sign)
+        vec.tensor_scalar_mul(out=lin[:, d], in0=lin[:, d], scalar1=-2.0 * sign)
+        vec.tensor_scalar_mul(out=con[:, d], in0=con[:, d], scalar1=sign)
+        inv_gain = new("inv_gain")
+        vec.reciprocal(out=inv_gain[:], in_=gain[:, d])
+        vec.scalar_tensor_tensor(out=bias[:, d], in0=lin[:, d], scalar=0.5, in1=inv_gain[:], op0=ALU.mult, op1=ALU.mult)
+        vec.tensor_sub(out=bias[:, d], in0=bias[:, d], in1=knot(2))
+
+    vec.tensor_copy(out=lo[:, 0], in_=knot(0))
+    vec.tensor_copy(out=hi[:, N_PIECE - 1], in_=knot(N_PIECE))
+    for d in range(1, N_PIECE):
+        values = []
+        for side in (d - 1, d):
+            val = new("val%d" % (side - d + 1))
+            vec.tensor_mul(out=val[:], in0=gain[:, side], in1=rel[d][:])
+            if side == d:
+                steep = new("steep")
+                vec.scalar_tensor_tensor(out=steep[:], in0=val[:], scalar=2.0, in1=lin[:, d], op0=ALU.mult, op1=ALU.add)
+            vec.tensor_add(out=val[:], in0=val[:], in1=lin[:, side])
+            vec.tensor_mul(out=val[:], in0=val[:], in1=rel[d][:])
+            vec.tensor_add(out=val[:], in0=val[:], in1=con[:, side])
+            values.append(val)
+        shift = new("shift")
+        vec.tensor_sub(out=shift[:], in0=values[1][:], in1=values[0][:])
+        vec.reciprocal(out=steep[:], in_=steep[:])
+        vec.tensor_mul(out=shift[:], in0=shift[:], in1=steep[:])
+        part = new("part")
+        vec.tensor_scalar_max(out=part[:], in0=shift[:], scalar1=0.0)
+        vec.tensor_sub(out=lo[:, d], in0=knot(d), in1=part[:])
+        vec.tensor_scalar_min(out=part[:], in0=shift[:], scalar1=0.0)
+        vec.tensor_add(out=hi[:, d - 1], in0=knot(d), in1=part[:])
+
+    for d in range(1, N_PIECE):
+        held = new("held")
+        vec.tensor_add(out=held[:], in0=lo[:, d], in1=bias[:, d])
+        vec.tensor_mul(out=held[:], in0=held[:], in1=held[:])
+        vec.scalar_tensor_tensor(out=held[:], in0=held[:], scalar=-1.0, in1=gain[:, d], op0=ALU.mult, op1=ALU.mult)
+        if d == 1:
+            vec.tensor_copy(out=offset[:], in_=held[:])
+        else:
+            vec.tensor_add(out=offset[:], in0=offset[:], in1=held[:])
+    return gain, bias, lo, hi, offset
+
+
+def tile_kanlayer_t_kernel(tc, x, base_weight, spline_weight, grid, grad_out, out):
+    nc = tc.nc
+    with ExitStack() as ctx:
+        keep = ctx.enter_context(tc.tile_pool(name="keep", bufs=1))
+        tabs = ctx.enter_context(tc.tile_pool(name="tabs", bufs=1))
+        tmp = ctx.enter_context(tc.tile_pool(name="tmp", bufs=2))
+        work = ctx.enter_context(tc.tile_pool(name="work", bufs=3))
+        psum_c = ctx.enter_context(tc.psum_pool(name="psum_c", bufs=4))
+        psum_o = ctx.enter_context(tc.psum_pool(name="psum_o", bufs=2))
+
+        ident_bf = keep.tile([P, P], BF16, name="ident_bf")
+        make_identity(nc, ident_bf[:])
+        ident_f = keep.tile([P, P], F32, name="ident_f")
+        make_identity(nc, ident_f[:])
+
+        x_t = keep.tile([P, N_IB, B], BF16, name="x_t")
+        w_codes = keep.tile([P, N_C + 1, IN], U32, name="w_codes", align_bytes=64)
+        w_scales = keep.tile([P, N_C + 1, IN], U8, name="w_scales", align_bytes=64)
+        g_codes = keep.tile([P, B], U32, name="g_codes", align_bytes=64)
+        g_scales = keep.tile([P, B], U8, name="g_scales", align_bytes=64)
+
+        with tc.tile_pool(name="load", bufs=1) as load, tc.tile_pool(name="regroup", bufs=2) as regroup, tc.psum_pool(
+            name="psum_s", bufs=2
+        ) as psum_s:
+            kn_bf = load.tile([P, N_IB, N_KNOTS], BF16, name="kn_bf")
+            nc.sync.dma_start(out=kn_bf[:], in_=grid.rearrange("(n p) k -> p n k", p=P))
+            x_sb = load.tile([P, N_TB, IN], BF16, name="x_sb")
+            nc.sync.dma_start(out=x_sb[:], in_=x.rearrange("(t p) i -> p t i", p=P))
+            g_sb = load.tile([P, N_TB, OUT], BF16, name="g_sb")
+            nc.sync.dma_start(out=g_sb[:], in_=grad_out.rearrange("(t p) o -> p t o", p=P))
+            b_raw = load.tile([P, PACK, IN], BF16, name="b_raw")
+            nc.sync.dma_start(out=b_raw[:], in_=base_weight.rearrange("(p j) i -> p j i", j=PACK))
+            w_raw = load.tile([P, PACK, IN * N_C], BF16, name="w_raw")
+            nc.sync.dma_start(out=w_raw[:], in_=spline_weight.rearrange("(p j) i c -> p j (i c)", j=PACK))
+
+            kn = tabs.tile([P, N_IB, N_KNOTS], F32, name="kn")
+            nc.vector.tensor_copy(out=kn[:], in_=kn_bf[:])
+            gain, bias, lo, hi, offset = spline_tables(nc, tabs, tmp, kn)
+
+            for ib in range(N_IB):
+                for half in range(2):
+                    xt_ps = psum_s.tile([P, 8, P], BF16, name="xt_ps", tag="setup")
+                    for t in range(8):
+                        nc.tensor.transpose(xt_ps[:, t, :], x_sb[:, half * 8 + t, ib * P : (ib + 1) * P], ident_bf[:])
+                    nc.scalar.copy(
+                        out=x_t[:, ib, half * 8 * P : (half + 1) * 8 * P], in_=xt_ps[:].rearrange("p t k -> p (t k)")
+                    )
+
+            g_words = g_sb[:].bitcast(F32).rearrange("p t (w u) -> p t u w", u=2)
+            g_grp = load.tile([P, B, PACK], BF16, name="g_grp", align_bytes=64)
+            grp_words = g_grp[:].bitcast(F32)
+            for pair in range(N_TB // 2):
+                gt_ps = psum_s.tile([P, 2, 2, P], F32, name="gt_ps", tag="setup")
+                for t in range(2):
+                    for u in range(2):
+                        nc.tensor.transpose(gt_ps[:, t, u, :], g_words[:, 2 * pair + t, u, :], ident_f[:])
+                nc.vector.tensor_copy(
+                    out=grp_words[:, pair * 2 * P : (pair + 1) * 2 * P, :].rearrange("p (t k) u -> p t k u", t=2),
+                    in_=gt_ps[:].rearrange("p t u k -> p t k u"),
+                )
+            for half in range(2):
+                toks = slice(half * (B // 2), (half + 1) * (B // 2))
+                nc.vector.quantize_mx(
+                    out=g_codes[:, toks].bitcast(E5M2X4),
+                    scales=g_scales[:, toks],
+                    in_=g_grp[:, toks, :].rearrange("p k t -> p (k t)"),
+                )
+
+            w_by_c = w_raw[:].rearrange("p j (i c) -> p c i j", c=N_C)
+            for c in range(N_C + 1):
+                w_grp = regroup.tile([P, IN, PACK], BF16, name="w_grp", align_bytes=64)
+                if c < N_C:
+                    nc.scalar.copy(out=w_grp[:], in_=w_by_c[:, c])
+                else:
+                    nc.scalar.copy(out=w_grp[:], in_=b_raw[:].rearrange("p j i -> p i j"))
+                nc.vector.quantize_mx(
+                    out=w_codes[:, c, :].bitcast(E4M3X4),
+                    scales=w_scales[:, c, :],
+                    in_=w_grp[:].rearrange("p i j -> p (i j)"),
+                )
+
+        terms = ctx.enter_context(tc.tile_pool(name="terms", bufs=1))
+        out_rows = out.rearrange("(q t p) f -> q p t f", t=TB_PER_BANK, p=P)
+
+        for ib in range(N_IB):
+            feats = slice(ib * P, (ib + 1) * P)
+            term = []
+            for c in range(N_C + 1):
+                sums = []
+                for ch in range(N_CHUNK):
+                    toks = slice(ch * CHUNK, (ch + 1) * CHUNK)
+                    c_ps = psum_c.tile([P, CHUNK], F32, name="c_ps")
+                    nc.tensor.matmul_mx(
+                        out=c_ps[:],
+                        lhsT=w_codes[:, c, feats].bitcast(E4M3X4),
+                        lhsT_scale=w_scales[:, c, feats],
+                        rhs=g_codes[:, toks].bitcast(E5M2X4),
+                        rhs_scale=g_scales[:, toks],
+                        start=True,
+                        stop=True,
+                    )
+                    sums.append(c_ps)
+                prod = terms.tile([P, B], F32, name="prod%d" % c)
+                term.append(prod)
+                if c < N_C:
+                    slope = work.tile([P, B], F32, name="slope")
+                    for d in range(N_PIECE):
+                        one = slice(c, c + 1)
+                        u = work.tile([P, B], BF16, name="u")
+                        nc.vector.tensor_scalar(
+                            out=u[:], in0=x_t[:, ib, :], scalar1=lo[:, d, ib, one], scalar2=hi[:, d, ib, one],
+                            op0=ALU.max, op1=ALU.min,
+                        )
+                        sq = work.tile([P, B], F32, name="sq")
+                        nc.scalar.activation(out=sq[:], in_=u[:], func=ACT.Square, bias=bias[:, d, ib, one], scale=1.0)
+                        if d == 0:
+                            nc.vector.tensor_scalar(
+                                out=slope[:], in0=sq[:], scalar1=gain[:, d, ib, one], scalar2=offset[:, ib, one],
+                                op0=ALU.mult, op1=ALU.add,
+                            )
+                        else:
+                            nc.vector.scalar_tensor_tensor(
+                                out=slope[:], in0=sq[:], scalar=gain[:, d, ib, one], in1=slope[:],
+                                op0=ALU.mult, op1=ALU.add,
+                            )
+                    for ch in range(N_CHUNK):
+                        toks = slice(ch * CHUNK, (ch + 1) * CHUNK)
+                        nc.vector.tensor_tensor(out=prod[:, toks], in0=slope[:, toks], in1=sums[ch][:], op=ALU.mult)
+                else:
+                    for ch in range(N_CHUNK):
+                        toks = slice(ch * CHUNK, (ch + 1) * CHUNK)
+                        nc.scalar.copy(out=prod[:, toks], in_=sums[ch][:])
+
+            for q in range(N_TB // TB_PER_BANK):
+                o_ps = psum_o.tile([P, TB_PER_BANK, P], F32, name="o_ps")
+                for t in range(TB_PER_BANK):
+                    tb = q * TB_PER_BANK + t
+                    for c in range(N_C + 1):
+                        nc.tensor.matmul(
+                            o_ps[:, t, :], lhsT=term[c][:, tb * P : (tb + 1) * P], rhs=ident_f[:],
+                            is_transpose=True, start=(c == 0), stop=(c == N_C),
+                        )
+                o_sb = work.tile([P, TB_PER_BANK, P], F32, name="o_sb")
+                nc.scalar.copy(out=o_sb[:], in_=o_ps[:])
+                nc.sync.dma_start(out=out_rows[q][:, :, feats], in_=o_sb[:])

@@ -26,6 +26,9 @@ N_TB = B // P
 CHUNK = 512
 N_CHUNK = B // CHUNK
 TB_PER_BANK = CHUNK // P
+UPWARD = (0, 2)
+LOAD_TB = 4
+STORE_AT = 2
 
 FLOPS = 2 * B * OUT * IN * (N_C + 1)
 
@@ -135,7 +138,18 @@ def spline_tables(nc, tabs, tmp, kn):
             vec.tensor_copy(out=offset[:], in_=held[:])
         else:
             vec.tensor_add(out=offset[:], in0=offset[:], in1=held[:])
-    return gain, bias, lo, hi, offset
+
+    root = tabs.tile([P, N_PIECE, N_IB, N_C], F32, name="root")
+    root_bias = tabs.tile([P, N_PIECE, N_IB, N_C], F32, name="root_bias")
+    for d in UPWARD:
+        nc.scalar.sqrt(out=root[:, d], in_=gain[:, d])
+        ratio = new("ratio")
+        vec.reciprocal(out=ratio[:], in_=root[:, d])
+        vec.tensor_mul(out=ratio[:], in0=ratio[:], in1=gain[:, d])
+        vec.tensor_add(out=root[:, d], in0=root[:, d], in1=ratio[:])
+        vec.tensor_scalar_mul(out=root[:, d], in0=root[:, d], scalar1=0.5)
+        vec.tensor_mul(out=root_bias[:, d], in0=root[:, d], in1=bias[:, d])
+    return gain, bias, lo, hi, offset, root, root_bias
 
 
 def tile_kanlayer_t_kernel(tc, x, base_weight, spline_weight, grid, grad_out, out):
@@ -144,9 +158,11 @@ def tile_kanlayer_t_kernel(tc, x, base_weight, spline_weight, grid, grad_out, ou
         keep = ctx.enter_context(tc.tile_pool(name="keep", bufs=1))
         tabs = ctx.enter_context(tc.tile_pool(name="tabs", bufs=1))
         tmp = ctx.enter_context(tc.tile_pool(name="tmp", bufs=2))
-        work = ctx.enter_context(tc.tile_pool(name="work", bufs=3))
+        clamped = ctx.enter_context(tc.tile_pool(name="clamped", bufs=6))
+        squares = ctx.enter_context(tc.tile_pool(name="squares", bufs=7))
+        rows = ctx.enter_context(tc.tile_pool(name="rows", bufs=2))
         psum_c = ctx.enter_context(tc.psum_pool(name="psum_c", bufs=4))
-        psum_o = ctx.enter_context(tc.psum_pool(name="psum_o", bufs=2))
+        psum_t = ctx.enter_context(tc.psum_pool(name="psum_t", bufs=4))
 
         ident_bf = keep.tile([P, P], BF16, name="ident_bf")
         make_identity(nc, ident_bf[:])
@@ -159,15 +175,21 @@ def tile_kanlayer_t_kernel(tc, x, base_weight, spline_weight, grid, grad_out, ou
         g_codes = keep.tile([P, B], U32, name="g_codes", align_bytes=64)
         g_scales = keep.tile([P, B], U8, name="g_scales", align_bytes=64)
 
-        with tc.tile_pool(name="load", bufs=1) as load, tc.tile_pool(name="regroup", bufs=2) as regroup, tc.psum_pool(
-            name="psum_s", bufs=2
-        ) as psum_s:
+        with tc.tile_pool(name="load", bufs=1) as load, tc.tile_pool(name="stream", bufs=2) as stream:
             kn_bf = load.tile([P, N_IB, N_KNOTS], BF16, name="kn_bf")
             nc.sync.dma_start(out=kn_bf[:], in_=grid.rearrange("(n p) k -> p n k", p=P))
-            x_sb = load.tile([P, N_TB, IN], BF16, name="x_sb")
-            nc.sync.dma_start(out=x_sb[:], in_=x.rearrange("(t p) i -> p t i", p=P))
-            g_sb = load.tile([P, N_TB, OUT], BF16, name="g_sb")
-            nc.sync.dma_start(out=g_sb[:], in_=grad_out.rearrange("(t p) o -> p t o", p=P))
+            x_blocks = x.rearrange("(l t p) i -> l p t i", t=LOAD_TB, p=P)
+            g_blocks = grad_out.rearrange("(l t p) o -> l p t o", t=LOAD_TB, p=P)
+            x_sbs = []
+            for l in range(N_TB // LOAD_TB):
+                x_sb = load.tile([P, LOAD_TB, IN], BF16, name="x_sb%d" % l)
+                nc.sync.dma_start(out=x_sb[:], in_=x_blocks[l])
+                x_sbs.append(x_sb)
+            g_sbs = []
+            for l in range(N_TB // LOAD_TB):
+                g_sb = stream.tile([P, LOAD_TB, OUT], BF16, name="g_sb")
+                nc.sync.dma_start(out=g_sb[:], in_=g_blocks[l])
+                g_sbs.append(g_sb)
             b_raw = load.tile([P, PACK, IN], BF16, name="b_raw")
             nc.sync.dma_start(out=b_raw[:], in_=base_weight.rearrange("(p j) i -> p j i", j=PACK))
             w_raw = load.tile([P, PACK, IN * N_C], BF16, name="w_raw")
@@ -175,40 +197,43 @@ def tile_kanlayer_t_kernel(tc, x, base_weight, spline_weight, grid, grad_out, ou
 
             kn = tabs.tile([P, N_IB, N_KNOTS], F32, name="kn")
             nc.vector.tensor_copy(out=kn[:], in_=kn_bf[:])
-            gain, bias, lo, hi, offset = spline_tables(nc, tabs, tmp, kn)
+            gain, bias, lo, hi, offset, root, root_bias = spline_tables(nc, tabs, tmp, kn)
 
             for ib in range(N_IB):
                 for half in range(2):
-                    xt_ps = psum_s.tile([P, 8, P], BF16, name="xt_ps", tag="setup")
+                    xt_ps = psum_t.tile([P, 8, P], BF16, name="xt_ps", tag="bank")
                     for t in range(8):
-                        nc.tensor.transpose(xt_ps[:, t, :], x_sb[:, half * 8 + t, ib * P : (ib + 1) * P], ident_bf[:])
+                        tb = half * 8 + t
+                        nc.tensor.transpose(
+                            xt_ps[:, t, :], x_sbs[tb // LOAD_TB][:, tb % LOAD_TB, ib * P : (ib + 1) * P], ident_bf[:]
+                        )
                     nc.scalar.copy(
                         out=x_t[:, ib, half * 8 * P : (half + 1) * 8 * P], in_=xt_ps[:].rearrange("p t k -> p (t k)")
                     )
 
-            g_words = g_sb[:].bitcast(F32).rearrange("p t (w u) -> p t u w", u=2)
-            g_grp = load.tile([P, B, PACK], BF16, name="g_grp", align_bytes=64)
-            grp_words = g_grp[:].bitcast(F32)
-            for pair in range(N_TB // 2):
-                gt_ps = psum_s.tile([P, 2, 2, P], F32, name="gt_ps", tag="setup")
-                for t in range(2):
-                    for u in range(2):
-                        nc.tensor.transpose(gt_ps[:, t, u, :], g_words[:, 2 * pair + t, u, :], ident_f[:])
-                nc.vector.tensor_copy(
-                    out=grp_words[:, pair * 2 * P : (pair + 1) * 2 * P, :].rearrange("p (t k) u -> p t k u", t=2),
-                    in_=gt_ps[:].rearrange("p t u k -> p t k u"),
-                )
-            for half in range(2):
-                toks = slice(half * (B // 2), (half + 1) * (B // 2))
+            for l in range(N_TB // LOAD_TB):
+                g_words = g_sbs[l][:].bitcast(F32).rearrange("p t (w u) -> p t u w", u=2)
+                g_grp = stream.tile([P, LOAD_TB * P, PACK], BF16, name="g_grp", align_bytes=64)
+                grp_words = g_grp[:].bitcast(F32)
+                for pair in range(LOAD_TB // 2):
+                    gt_ps = psum_t.tile([P, 2, 2, P], F32, name="gt_ps", tag="bank")
+                    for t in range(2):
+                        for u in range(2):
+                            nc.tensor.transpose(gt_ps[:, t, u, :], g_words[:, 2 * pair + t, u, :], ident_f[:])
+                    nc.scalar.copy(
+                        out=grp_words[:, pair * 2 * P : (pair + 1) * 2 * P, :].rearrange("p (t k) u -> p t k u", t=2),
+                        in_=gt_ps[:].rearrange("p t u k -> p t k u"),
+                    )
+                toks = slice(l * LOAD_TB * P, (l + 1) * LOAD_TB * P)
                 nc.vector.quantize_mx(
                     out=g_codes[:, toks].bitcast(E5M2X4),
                     scales=g_scales[:, toks],
-                    in_=g_grp[:, toks, :].rearrange("p k t -> p (k t)"),
+                    in_=g_grp[:].rearrange("p k t -> p (k t)"),
                 )
 
             w_by_c = w_raw[:].rearrange("p j (i c) -> p c i j", c=N_C)
-            for c in range(N_C + 1):
-                w_grp = regroup.tile([P, IN, PACK], BF16, name="w_grp", align_bytes=64)
+            for c in [N_C] + list(range(N_C)):
+                w_grp = stream.tile([P, IN, PACK], BF16, name="w_grp", align_bytes=64)
                 if c < N_C:
                     nc.scalar.copy(out=w_grp[:], in_=w_by_c[:, c])
                 else:
@@ -220,66 +245,110 @@ def tile_kanlayer_t_kernel(tc, x, base_weight, spline_weight, grid, grad_out, ou
                 )
 
         terms = ctx.enter_context(tc.tile_pool(name="terms", bufs=1))
+        bases = ctx.enter_context(tc.tile_pool(name="bases", bufs=2))
         out_rows = out.rearrange("(q t p) f -> q p t f", t=TB_PER_BANK, p=P)
+        chunks = [slice(ch * CHUNK, (ch + 1) * CHUNK) for ch in range(N_CHUNK)]
 
-        for ib in range(N_IB):
+        def clamp_and_square(ib, c, d):
+            one = slice(c, c + 1)
+            u = clamped.tile([P, B], BF16, name="u")
+            nc.vector.tensor_scalar(
+                out=u[:], in0=x_t[:, ib, :], scalar1=lo[:, d, ib, one], scalar2=hi[:, d, ib, one],
+                op0=ALU.max, op1=ALU.min,
+            )
+            sq = squares.tile([P, B], F32, name="sq")
+            if d in UPWARD:
+                nc.scalar.activation(
+                    out=sq[:], in_=u[:], func=ACT.Square, bias=root_bias[:, d, ib, one], scale=root[:, d, ib, one]
+                )
+            else:
+                nc.scalar.activation(out=sq[:], in_=u[:], func=ACT.Square, bias=bias[:, d, ib, one], scale=1.0)
+            return sq
+
+        def add_pair(ib, c, sq, d):
+            nc.vector.scalar_tensor_tensor(
+                out=sq[d][:], in0=sq[d + 1][:], scalar=gain[:, d + 1, ib, c : c + 1], in1=sq[d][:],
+                op0=ALU.mult, op1=ALU.add,
+            )
+
+        def mx_sums(ib, c):
             feats = slice(ib * P, (ib + 1) * P)
-            term = []
-            for c in range(N_C + 1):
-                sums = []
-                for ch in range(N_CHUNK):
-                    toks = slice(ch * CHUNK, (ch + 1) * CHUNK)
-                    c_ps = psum_c.tile([P, CHUNK], F32, name="c_ps")
-                    nc.tensor.matmul_mx(
-                        out=c_ps[:],
-                        lhsT=w_codes[:, c, feats].bitcast(E4M3X4),
-                        lhsT_scale=w_scales[:, c, feats],
-                        rhs=g_codes[:, toks].bitcast(E5M2X4),
-                        rhs_scale=g_scales[:, toks],
-                        start=True,
-                        stop=True,
-                    )
-                    sums.append(c_ps)
-                prod = terms.tile([P, B], F32, name="prod%d" % c)
-                term.append(prod)
-                if c < N_C:
-                    slope = work.tile([P, B], F32, name="slope")
-                    for d in range(N_PIECE):
-                        one = slice(c, c + 1)
-                        u = work.tile([P, B], BF16, name="u")
-                        nc.vector.tensor_scalar(
-                            out=u[:], in0=x_t[:, ib, :], scalar1=lo[:, d, ib, one], scalar2=hi[:, d, ib, one],
-                            op0=ALU.max, op1=ALU.min,
-                        )
-                        sq = work.tile([P, B], F32, name="sq")
-                        nc.scalar.activation(out=sq[:], in_=u[:], func=ACT.Square, bias=bias[:, d, ib, one], scale=1.0)
-                        if d == 0:
-                            nc.vector.tensor_scalar(
-                                out=slope[:], in0=sq[:], scalar1=gain[:, d, ib, one], scalar2=offset[:, ib, one],
-                                op0=ALU.mult, op1=ALU.add,
-                            )
-                        else:
-                            nc.vector.scalar_tensor_tensor(
-                                out=slope[:], in0=sq[:], scalar=gain[:, d, ib, one], in1=slope[:],
-                                op0=ALU.mult, op1=ALU.add,
-                            )
-                    for ch in range(N_CHUNK):
-                        toks = slice(ch * CHUNK, (ch + 1) * CHUNK)
-                        nc.vector.tensor_tensor(out=prod[:, toks], in0=slope[:, toks], in1=sums[ch][:], op=ALU.mult)
-                else:
-                    for ch in range(N_CHUNK):
-                        toks = slice(ch * CHUNK, (ch + 1) * CHUNK)
-                        nc.scalar.copy(out=prod[:, toks], in_=sums[ch][:])
+            sums = []
+            for toks in chunks:
+                c_ps = psum_c.tile([P, CHUNK], F32, name="c_ps")
+                nc.tensor.matmul_mx(
+                    out=c_ps[:],
+                    lhsT=w_codes[:, c, feats].bitcast(E4M3X4),
+                    lhsT_scale=w_scales[:, c, feats],
+                    rhs=g_codes[:, toks].bitcast(E5M2X4),
+                    rhs_scale=g_scales[:, toks],
+                    start=True,
+                    stop=True,
+                )
+                sums.append(c_ps)
+            return sums
 
+        def base_term(ib):
+            sums = mx_sums(ib, N_C)
+            base = bases.tile([P, B], F32, name="base")
+            for ch in range(N_CHUNK):
+                nc.scalar.copy(out=base[:, chunks[ch]], in_=sums[ch][:])
+            return base
+
+        def add_terms(term):
+            banks = []
             for q in range(N_TB // TB_PER_BANK):
-                o_ps = psum_o.tile([P, TB_PER_BANK, P], F32, name="o_ps")
+                o_ps = psum_t.tile([P, TB_PER_BANK, P], F32, name="o_ps", tag="bank")
                 for t in range(TB_PER_BANK):
                     tb = q * TB_PER_BANK + t
-                    for c in range(N_C + 1):
+                    for n in range(N_C + 1):
                         nc.tensor.matmul(
-                            o_ps[:, t, :], lhsT=term[c][:, tb * P : (tb + 1) * P], rhs=ident_f[:],
-                            is_transpose=True, start=(c == 0), stop=(c == N_C),
+                            o_ps[:, t, :], lhsT=term[n][:, tb * P : (tb + 1) * P], rhs=ident_f[:],
+                            is_transpose=True, start=(n == 0), stop=(n == N_C),
                         )
-                o_sb = work.tile([P, TB_PER_BANK, P], F32, name="o_sb")
-                nc.scalar.copy(out=o_sb[:], in_=o_ps[:])
-                nc.sync.dma_start(out=out_rows[q][:, :, feats], in_=o_sb[:])
+                banks.append(o_ps)
+            return banks
+
+        def store(ib, banks):
+            for q in range(N_TB // TB_PER_BANK):
+                o_sb = rows.tile([P, TB_PER_BANK, P], F32, name="o_sb")
+                nc.scalar.copy(out=o_sb[:], in_=banks[q][:])
+                nc.sync.dma_start(out=out_rows[q][:, :, ib * P : (ib + 1) * P], in_=o_sb[:])
+
+        units = [(ib, c) for ib in range(N_IB) for c in range(N_C)]
+        with tc.manual_schedule():
+            sq_next = [clamp_and_square(0, 0, d) for d in range(N_PIECE)]
+            term = [base_term(0)]
+            sums_next = mx_sums(0, 0)
+            waiting = []
+            for k in range(len(units)):
+                ib, c = units[k]
+                sq, sums = sq_next, sums_next
+                ahead = units[k + 1 : k + 2]
+                sq_next = [clamp_and_square(i, n, 0) for i, n in ahead]
+                add_pair(ib, c, sq, 0)
+                sq_next += [clamp_and_square(i, n, 1) for i, n in ahead]
+                add_pair(ib, c, sq, 2)
+                sq_next += [clamp_and_square(i, n, 2) for i, n in ahead]
+                nc.vector.tensor_add(out=sq[0][:], in0=sq[0][:], in1=sq[2][:])
+                sq_next += [clamp_and_square(i, n, 3) for i, n in ahead]
+                prod = terms.tile([P, B], F32, name="prod%d" % c)
+                for ch in range(N_CHUNK):
+                    nc.vector.scalar_tensor_tensor(
+                        out=prod[:, chunks[ch]], in0=sq[0][:, chunks[ch]], scalar=offset[:, ib, c : c + 1],
+                        in1=sums[ch][:], op0=ALU.add, op1=ALU.mult,
+                    )
+                term.append(prod)
+                if c == STORE_AT:
+                    for done_ib, banks in waiting:
+                        store(done_ib, banks)
+                    waiting = []
+                full = term
+                if c == N_C - 1 and ib + 1 < N_IB:
+                    term = [base_term(ib + 1)]
+                for i, n in ahead:
+                    sums_next = mx_sums(i, n)
+                if c == N_C - 1:
+                    waiting = [(ib, add_terms(full))]
+            for done_ib, banks in waiting:
+                store(done_ib, banks)

@@ -28,126 +28,154 @@ N_CHUNK = B // CHUNK
 TB_PER_BANK = CHUNK // P
 UPWARD = (0, 2)
 LOAD_TB = 4
+BASE_AT = 3
 STORE_AT = 2
+SPARE_TERMS = 2
 
 FLOPS = 2 * B * OUT * IN * (N_C + 1)
 
 PATHS = (
-    (1.0, ((0, 0, 0, (0, 0, 0)),)),
-    (-1.0, ((0, 0, 1, (0, 0, 2)), (0, 1, 1, (0, 3, 1)), (1, 1, 1, (4, 1, 1)))),
-    (1.0, ((0, 1, 2, (0, 3, 3)), (1, 1, 2, (4, 1, 3)), (1, 2, 2, (4, 4, 2)))),
-    (-1.0, ((1, 2, 3, (4, 4, 4)),)),
+    (0, 0, 0, 0, (0, 0, 0)),
+    (1, 0, 0, 1, (0, 0, 2)),
+    (1, 0, 1, 1, (0, 3, 1)),
+    (1, 1, 1, 1, (4, 1, 1)),
+    (2, 0, 1, 2, (0, 3, 3)),
+    (2, 1, 1, 2, (4, 1, 3)),
+    (2, 1, 2, 2, (4, 4, 2)),
+    (3, 1, 2, 3, (4, 4, 4)),
 )
+SIGN = (1.0, -1.0, 1.0, -1.0)
 
 
-def spline_tables(nc, tabs, tmp, kn):
+def spline_tables(nc, tabs, kn):
     vec = nc.vector
 
     def knot(e):
         return kn[:, :, e : e + N_C]
 
-    def new(name):
-        return tmp.tile([P, N_IB, N_C], F32, name=name)
+    def table(name):
+        return tabs.tile([P, N_IB, N_C], F32, name=name)
 
-    inv_span = {}
-    for s in (1, 2, 3):
-        n = N_KNOTS - s
-        inv = tabs.tile([P, N_IB, n], F32, name="inv_span%d" % s)
-        vec.tensor_sub(out=inv[:], in0=kn[:, :, s:N_KNOTS], in1=kn[:, :, 0:n])
-        vec.tensor_scalar_add(out=inv[:], in0=inv[:], scalar1=EPS)
-        vec.reciprocal(out=inv[:], in_=inv[:])
-        inv_span[s] = inv
+    def per_piece(name):
+        return tabs.tile([P, N_PIECE, N_IB, N_C], F32, name=name)
 
-    rel = []
+    spans = (1, 2, 3)
+    inv_span = {s: tabs.tile([P, N_IB, N_KNOTS - s], F32, name="inv_span%d" % s) for s in spans}
+    for s in spans:
+        vec.tensor_sub(out=inv_span[s][:], in0=kn[:, :, s:N_KNOTS], in1=kn[:, :, 0 : N_KNOTS - s])
+    for s in spans:
+        vec.tensor_scalar_add(out=inv_span[s][:], in0=inv_span[s][:], scalar1=EPS)
+    for s in spans:
+        vec.reciprocal(out=inv_span[s][:], in_=inv_span[s][:])
+
+    rel = [table("rel%d" % e) for e in range(5)]
     for e in range(5):
-        r = tabs.tile([P, N_IB, N_C], F32, name="rel%d" % e)
-        vec.tensor_sub(out=r[:], in0=knot(e), in1=knot(2))
-        rel.append(r)
+        vec.tensor_sub(out=rel[e][:], in0=knot(e), in1=knot(2))
 
-    gain = tabs.tile([P, N_PIECE, N_IB, N_C], F32, name="gain")
-    lin = tabs.tile([P, N_PIECE, N_IB, N_C], F32, name="lin")
-    con = tabs.tile([P, N_PIECE, N_IB, N_C], F32, name="con")
-    bias = tabs.tile([P, N_PIECE, N_IB, N_C], F32, name="bias")
-    lo = tabs.tile([P, N_PIECE, N_IB, N_C], F32, name="lo")
-    hi = tabs.tile([P, N_PIECE, N_IB, N_C], F32, name="hi")
-    offset = tabs.tile([P, N_IB, N_C], F32, name="offset")
+    n_paths = range(len(PATHS))
+    k = [table("k%d" % n) for n in n_paths]
+    pair = [table("pair%d" % n) for n in n_paths]
+    sum1 = [table("sum1_%d" % n) for n in n_paths]
+    sum2 = [table("sum2_%d" % n) for n in n_paths]
+    cross = [table("cross%d" % n) for n in n_paths]
+    for n, (d, e3, e2, e1, (a, b, c)) in enumerate(PATHS):
+        vec.tensor_mul(out=k[n][:], in0=inv_span[3][:, :, e3 : e3 + N_C], in1=inv_span[2][:, :, e2 : e2 + N_C])
+    for n, (d, e3, e2, e1, (a, b, c)) in enumerate(PATHS):
+        vec.tensor_add(out=pair[n][:], in0=rel[a][:], in1=rel[b][:])
+    for n, (d, e3, e2, e1, (a, b, c)) in enumerate(PATHS):
+        vec.tensor_mul(out=k[n][:], in0=k[n][:], in1=inv_span[1][:, :, e1 : e1 + N_C])
+    for n, (d, e3, e2, e1, (a, b, c)) in enumerate(PATHS):
+        vec.tensor_mul(out=sum2[n][:], in0=rel[a][:], in1=rel[b][:])
+    for n, (d, e3, e2, e1, (a, b, c)) in enumerate(PATHS):
+        vec.tensor_add(out=sum1[n][:], in0=pair[n][:], in1=rel[c][:])
+    for n, (d, e3, e2, e1, (a, b, c)) in enumerate(PATHS):
+        vec.tensor_mul(out=cross[n][:], in0=pair[n][:], in1=rel[c][:])
+    for n in n_paths:
+        vec.tensor_mul(out=sum1[n][:], in0=sum1[n][:], in1=k[n][:])
+    for n in n_paths:
+        vec.tensor_add(out=sum2[n][:], in0=sum2[n][:], in1=cross[n][:])
+    for n in n_paths:
+        vec.tensor_mul(out=sum2[n][:], in0=sum2[n][:], in1=k[n][:])
 
+    gain = per_piece("gain")
+    lin = per_piece("lin")
+    con = per_piece("con")
+    parts = ((gain, k, 3.0), (lin, sum1, -2.0), (con, sum2, 1.0))
+    first = [[p[0] for p in PATHS].index(d) for d in range(N_PIECE)]
     for d in range(N_PIECE):
-        sign, paths = PATHS[d]
-        for n, (e3, e2, e1, (a, b, c)) in enumerate(paths):
-            k = new("k")
-            vec.tensor_mul(out=k[:], in0=inv_span[3][:, :, e3 : e3 + N_C], in1=inv_span[2][:, :, e2 : e2 + N_C])
-            vec.tensor_mul(out=k[:], in0=k[:], in1=inv_span[1][:, :, e1 : e1 + N_C])
-            pair = new("pair")
-            vec.tensor_add(out=pair[:], in0=rel[a][:], in1=rel[b][:])
-            sum1 = new("sum1")
-            vec.tensor_add(out=sum1[:], in0=pair[:], in1=rel[c][:])
-            sum2 = new("sum2")
-            vec.tensor_mul(out=sum2[:], in0=rel[a][:], in1=rel[b][:])
-            cross = new("cross")
-            vec.tensor_mul(out=cross[:], in0=pair[:], in1=rel[c][:])
-            vec.tensor_add(out=sum2[:], in0=sum2[:], in1=cross[:])
-            if n == 0:
-                vec.tensor_copy(out=gain[:, d], in_=k[:])
-                vec.tensor_mul(out=lin[:, d], in0=k[:], in1=sum1[:])
-                vec.tensor_mul(out=con[:, d], in0=k[:], in1=sum2[:])
-            else:
-                vec.tensor_add(out=gain[:, d], in0=gain[:, d], in1=k[:])
-                vec.tensor_mul(out=sum1[:], in0=k[:], in1=sum1[:])
-                vec.tensor_add(out=lin[:, d], in0=lin[:, d], in1=sum1[:])
-                vec.tensor_mul(out=sum2[:], in0=k[:], in1=sum2[:])
-                vec.tensor_add(out=con[:, d], in0=con[:, d], in1=sum2[:])
-        vec.tensor_scalar_mul(out=gain[:, d], in0=gain[:, d], scalar1=3.0 * sign)
-        vec.tensor_scalar_mul(out=lin[:, d], in0=lin[:, d], scalar1=-2.0 * sign)
-        vec.tensor_scalar_mul(out=con[:, d], in0=con[:, d], scalar1=sign)
-        inv_gain = new("inv_gain")
-        vec.reciprocal(out=inv_gain[:], in_=gain[:, d])
-        vec.scalar_tensor_tensor(out=bias[:, d], in0=lin[:, d], scalar=0.5, in1=inv_gain[:], op0=ALU.mult, op1=ALU.mult)
+        for total, part, factor in parts:
+            vec.tensor_scalar_mul(out=total[:, d], in0=part[first[d]][:], scalar1=factor * SIGN[d])
+    for n, path in enumerate(PATHS):
+        d = path[0]
+        if n != first[d]:
+            for total, part, factor in parts:
+                vec.scalar_tensor_tensor(
+                    out=total[:, d], in0=part[n][:], scalar=factor * SIGN[d], in1=total[:, d],
+                    op0=ALU.mult, op1=ALU.add,
+                )
+
+    bias = per_piece("bias")
+    inv_gain = per_piece("inv_gain")
+    vec.reciprocal(out=inv_gain[:], in_=gain[:])
+    vec.scalar_tensor_tensor(out=bias[:], in0=lin[:], scalar=0.5, in1=inv_gain[:], op0=ALU.mult, op1=ALU.mult)
+    for d in range(N_PIECE):
         vec.tensor_sub(out=bias[:, d], in0=bias[:, d], in1=knot(2))
 
+    lo = per_piece("lo")
+    hi = per_piece("hi")
     vec.tensor_copy(out=lo[:, 0], in_=knot(0))
     vec.tensor_copy(out=hi[:, N_PIECE - 1], in_=knot(N_PIECE))
-    for d in range(1, N_PIECE):
-        values = []
-        for side in (d - 1, d):
-            val = new("val%d" % (side - d + 1))
-            vec.tensor_mul(out=val[:], in0=gain[:, side], in1=rel[d][:])
-            if side == d:
-                steep = new("steep")
-                vec.scalar_tensor_tensor(out=steep[:], in0=val[:], scalar=2.0, in1=lin[:, d], op0=ALU.mult, op1=ALU.add)
-            vec.tensor_add(out=val[:], in0=val[:], in1=lin[:, side])
-            vec.tensor_mul(out=val[:], in0=val[:], in1=rel[d][:])
-            vec.tensor_add(out=val[:], in0=val[:], in1=con[:, side])
-            values.append(val)
-        shift = new("shift")
-        vec.tensor_sub(out=shift[:], in0=values[1][:], in1=values[0][:])
-        vec.reciprocal(out=steep[:], in_=steep[:])
-        vec.tensor_mul(out=shift[:], in0=shift[:], in1=steep[:])
-        part = new("part")
-        vec.tensor_scalar_max(out=part[:], in0=shift[:], scalar1=0.0)
-        vec.tensor_sub(out=lo[:, d], in0=knot(d), in1=part[:])
-        vec.tensor_scalar_min(out=part[:], in0=shift[:], scalar1=0.0)
-        vec.tensor_add(out=hi[:, d - 1], in0=knot(d), in1=part[:])
+    inner = range(1, N_PIECE)
+    left = {d: table("left%d" % d) for d in inner}
+    right = {d: table("right%d" % d) for d in inner}
+    steep = {d: table("steep%d" % d) for d in inner}
+    for d in inner:
+        vec.tensor_mul(out=left[d][:], in0=gain[:, d - 1], in1=rel[d][:])
+        vec.tensor_mul(out=right[d][:], in0=gain[:, d], in1=rel[d][:])
+    for d in inner:
+        vec.scalar_tensor_tensor(out=steep[d][:], in0=right[d][:], scalar=2.0, in1=lin[:, d], op0=ALU.mult, op1=ALU.add)
+        vec.tensor_add(out=left[d][:], in0=left[d][:], in1=lin[:, d - 1])
+        vec.tensor_add(out=right[d][:], in0=right[d][:], in1=lin[:, d])
+    for d in inner:
+        vec.reciprocal(out=steep[d][:], in_=steep[d][:])
+        vec.tensor_mul(out=left[d][:], in0=left[d][:], in1=rel[d][:])
+        vec.tensor_mul(out=right[d][:], in0=right[d][:], in1=rel[d][:])
+    for d in inner:
+        vec.tensor_add(out=left[d][:], in0=left[d][:], in1=con[:, d - 1])
+        vec.tensor_add(out=right[d][:], in0=right[d][:], in1=con[:, d])
+    for d in inner:
+        vec.tensor_sub(out=right[d][:], in0=right[d][:], in1=left[d][:])
+    for d in inner:
+        vec.tensor_mul(out=right[d][:], in0=right[d][:], in1=steep[d][:])
+    for d in inner:
+        vec.tensor_scalar_max(out=left[d][:], in0=right[d][:], scalar1=0.0)
+        vec.tensor_scalar_min(out=right[d][:], in0=right[d][:], scalar1=0.0)
+    for d in inner:
+        vec.tensor_sub(out=lo[:, d], in0=knot(d), in1=left[d][:])
+        vec.tensor_add(out=hi[:, d - 1], in0=knot(d), in1=right[d][:])
 
-    for d in range(1, N_PIECE):
-        held = new("held")
-        vec.tensor_add(out=held[:], in0=lo[:, d], in1=bias[:, d])
-        vec.tensor_mul(out=held[:], in0=held[:], in1=held[:])
-        vec.scalar_tensor_tensor(out=held[:], in0=held[:], scalar=-1.0, in1=gain[:, d], op0=ALU.mult, op1=ALU.mult)
-        if d == 1:
-            vec.tensor_copy(out=offset[:], in_=held[:])
-        else:
-            vec.tensor_add(out=offset[:], in0=offset[:], in1=held[:])
+    offset = table("offset")
+    held = per_piece("held")
+    vec.tensor_add(out=held[:], in0=lo[:], in1=bias[:])
+    vec.tensor_mul(out=held[:], in0=held[:], in1=held[:])
+    vec.scalar_tensor_tensor(out=held[:], in0=held[:], scalar=-1.0, in1=gain[:], op0=ALU.mult, op1=ALU.mult)
+    vec.tensor_add(out=offset[:], in0=held[:, 1], in1=held[:, 2])
+    vec.tensor_add(out=offset[:], in0=offset[:], in1=held[:, 3])
 
-    root = tabs.tile([P, N_PIECE, N_IB, N_C], F32, name="root")
-    root_bias = tabs.tile([P, N_PIECE, N_IB, N_C], F32, name="root_bias")
+    root = per_piece("root")
+    root_bias = per_piece("root_bias")
+    ratio = per_piece("ratio")
     for d in UPWARD:
         nc.scalar.sqrt(out=root[:, d], in_=gain[:, d])
-        ratio = new("ratio")
-        vec.reciprocal(out=ratio[:], in_=root[:, d])
-        vec.tensor_mul(out=ratio[:], in0=ratio[:], in1=gain[:, d])
-        vec.tensor_add(out=root[:, d], in0=root[:, d], in1=ratio[:])
+    for d in UPWARD:
+        vec.reciprocal(out=ratio[:, d], in_=root[:, d])
+    for d in UPWARD:
+        vec.tensor_mul(out=ratio[:, d], in0=ratio[:, d], in1=gain[:, d])
+    for d in UPWARD:
+        vec.tensor_add(out=root[:, d], in0=root[:, d], in1=ratio[:, d])
+    for d in UPWARD:
         vec.tensor_scalar_mul(out=root[:, d], in0=root[:, d], scalar1=0.5)
+    for d in UPWARD:
         vec.tensor_mul(out=root_bias[:, d], in0=root[:, d], in1=bias[:, d])
     return gain, bias, lo, hi, offset, root, root_bias
 
@@ -157,9 +185,8 @@ def tile_kanlayer_t_kernel(tc, x, base_weight, spline_weight, grid, grad_out, ou
     with ExitStack() as ctx:
         keep = ctx.enter_context(tc.tile_pool(name="keep", bufs=1))
         tabs = ctx.enter_context(tc.tile_pool(name="tabs", bufs=1))
-        tmp = ctx.enter_context(tc.tile_pool(name="tmp", bufs=2))
-        clamped = ctx.enter_context(tc.tile_pool(name="clamped", bufs=6))
-        squares = ctx.enter_context(tc.tile_pool(name="squares", bufs=7))
+        clamped = ctx.enter_context(tc.tile_pool(name="clamped", bufs=5))
+        squares = ctx.enter_context(tc.tile_pool(name="squares", bufs=6))
         rows = ctx.enter_context(tc.tile_pool(name="rows", bufs=2))
         psum_c = ctx.enter_context(tc.psum_pool(name="psum_c", bufs=4))
         psum_t = ctx.enter_context(tc.psum_pool(name="psum_t", bufs=4))
@@ -187,17 +214,18 @@ def tile_kanlayer_t_kernel(tc, x, base_weight, spline_weight, grid, grad_out, ou
                 x_sbs.append(x_sb)
             g_sbs = []
             for l in range(N_TB // LOAD_TB):
-                g_sb = stream.tile([P, LOAD_TB, OUT], BF16, name="g_sb")
+                g_sb = load.tile([P, LOAD_TB, OUT], BF16, name="g_sb%d" % l)
                 nc.sync.dma_start(out=g_sb[:], in_=g_blocks[l])
                 g_sbs.append(g_sb)
-            b_raw = load.tile([P, PACK, IN], BF16, name="b_raw")
-            nc.sync.dma_start(out=b_raw[:], in_=base_weight.rearrange("(p j) i -> p j i", j=PACK))
             w_raw = load.tile([P, PACK, IN * N_C], BF16, name="w_raw")
             nc.sync.dma_start(out=w_raw[:], in_=spline_weight.rearrange("(p j) i c -> p j (i c)", j=PACK))
+            b_raw = load.tile([P, PACK, IN], BF16, name="b_raw")
+            nc.sync.dma_start(out=b_raw[:], in_=base_weight.rearrange("(p j) i -> p j i", j=PACK))
 
             kn = tabs.tile([P, N_IB, N_KNOTS], F32, name="kn")
             nc.vector.tensor_copy(out=kn[:], in_=kn_bf[:])
-            gain, bias, lo, hi, offset, root, root_bias = spline_tables(nc, tabs, tmp, kn)
+            with tc.manual_schedule():
+                gain, bias, lo, hi, offset, root, root_bias = spline_tables(nc, tabs, kn)
 
             for ib in range(N_IB):
                 for half in range(2):
@@ -232,7 +260,7 @@ def tile_kanlayer_t_kernel(tc, x, base_weight, spline_weight, grid, grad_out, ou
                 )
 
             w_by_c = w_raw[:].rearrange("p j (i c) -> p c i j", c=N_C)
-            for c in [N_C] + list(range(N_C)):
+            for c in range(N_C + 1):
                 w_grp = stream.tile([P, IN, PACK], BF16, name="w_grp", align_bytes=64)
                 if c < N_C:
                     nc.scalar.copy(out=w_grp[:], in_=w_by_c[:, c])
@@ -244,10 +272,10 @@ def tile_kanlayer_t_kernel(tc, x, base_weight, spline_weight, grid, grad_out, ou
                     in_=w_grp[:].rearrange("p i j -> p (i j)"),
                 )
 
-        terms = ctx.enter_context(tc.tile_pool(name="terms", bufs=1))
-        bases = ctx.enter_context(tc.tile_pool(name="bases", bufs=2))
+        terms = ctx.enter_context(tc.tile_pool(name="terms", bufs=N_C + 1 + SPARE_TERMS))
         out_rows = out.rearrange("(q t p) f -> q p t f", t=TB_PER_BANK, p=P)
         chunks = [slice(ch * CHUNK, (ch + 1) * CHUNK) for ch in range(N_CHUNK)]
+        whole = slice(0, B)
 
         def clamp_and_square(ib, c, d):
             one = slice(c, c + 1)
@@ -265,10 +293,19 @@ def tile_kanlayer_t_kernel(tc, x, base_weight, spline_weight, grid, grad_out, ou
                 nc.scalar.activation(out=sq[:], in_=u[:], func=ACT.Square, bias=bias[:, d, ib, one], scale=1.0)
             return sq
 
-        def add_pair(ib, c, sq, d):
+        def add_pair(ib, c, sq, d, toks):
             nc.vector.scalar_tensor_tensor(
-                out=sq[d][:], in0=sq[d + 1][:], scalar=gain[:, d + 1, ib, c : c + 1], in1=sq[d][:],
+                out=sq[d][:, toks], in0=sq[d + 1][:, toks], scalar=gain[:, d + 1, ib, c : c + 1], in1=sq[d][:, toks],
                 op0=ALU.mult, op1=ALU.add,
+            )
+
+        def add_halves(sq, toks):
+            nc.vector.tensor_add(out=sq[0][:, toks], in0=sq[0][:, toks], in1=sq[2][:, toks])
+
+        def multiply(ib, c, sq, sums, prod, ch):
+            nc.vector.scalar_tensor_tensor(
+                out=prod[:, chunks[ch]], in0=sq[0][:, chunks[ch]], scalar=offset[:, ib, c : c + 1], in1=sums[ch][:],
+                op0=ALU.add, op1=ALU.mult,
             )
 
         def mx_sums(ib, c):
@@ -288,67 +325,64 @@ def tile_kanlayer_t_kernel(tc, x, base_weight, spline_weight, grid, grad_out, ou
                 sums.append(c_ps)
             return sums
 
-        def base_term(ib):
-            sums = mx_sums(ib, N_C)
-            base = bases.tile([P, B], F32, name="base")
-            for ch in range(N_CHUNK):
-                nc.scalar.copy(out=base[:, chunks[ch]], in_=sums[ch][:])
-            return base
+        def add_terms(term, q):
+            o_ps = psum_t.tile([P, TB_PER_BANK, P], F32, name="o_ps", tag="bank")
+            for t in range(TB_PER_BANK):
+                tb = q * TB_PER_BANK + t
+                for n in range(N_C + 1):
+                    nc.tensor.matmul(
+                        o_ps[:, t, :], lhsT=term[n][:, tb * P : (tb + 1) * P], rhs=ident_f[:],
+                        is_transpose=True, start=(n == 0), stop=(n == N_C),
+                    )
+            return o_ps
 
-        def add_terms(term):
-            banks = []
-            for q in range(N_TB // TB_PER_BANK):
-                o_ps = psum_t.tile([P, TB_PER_BANK, P], F32, name="o_ps", tag="bank")
-                for t in range(TB_PER_BANK):
-                    tb = q * TB_PER_BANK + t
-                    for n in range(N_C + 1):
-                        nc.tensor.matmul(
-                            o_ps[:, t, :], lhsT=term[n][:, tb * P : (tb + 1) * P], rhs=ident_f[:],
-                            is_transpose=True, start=(n == 0), stop=(n == N_C),
-                        )
-                banks.append(o_ps)
-            return banks
-
-        def store(ib, banks):
-            for q in range(N_TB // TB_PER_BANK):
-                o_sb = rows.tile([P, TB_PER_BANK, P], F32, name="o_sb")
-                nc.scalar.copy(out=o_sb[:], in_=banks[q][:])
-                nc.sync.dma_start(out=out_rows[q][:, :, ib * P : (ib + 1) * P], in_=o_sb[:])
+        def store(ib, q, o_ps):
+            o_sb = rows.tile([P, TB_PER_BANK, P], F32, name="o_sb")
+            nc.scalar.copy(out=o_sb[:], in_=o_ps[:])
+            nc.sync.dma_start(out=out_rows[q][:, :, ib * P : (ib + 1) * P], in_=o_sb[:])
 
         units = [(ib, c) for ib in range(N_IB) for c in range(N_C)]
+        last = len(units) - 1
         with tc.manual_schedule():
             sq_next = [clamp_and_square(0, 0, d) for d in range(N_PIECE)]
-            term = [base_term(0)]
             sums_next = mx_sums(0, 0)
+            term = []
             waiting = []
-            for k in range(len(units)):
+            for k in range(last):
                 ib, c = units[k]
+                ib_next, c_next = units[k + 1]
                 sq, sums = sq_next, sums_next
-                ahead = units[k + 1 : k + 2]
-                sq_next = [clamp_and_square(i, n, 0) for i, n in ahead]
-                add_pair(ib, c, sq, 0)
-                sq_next += [clamp_and_square(i, n, 1) for i, n in ahead]
-                add_pair(ib, c, sq, 2)
-                sq_next += [clamp_and_square(i, n, 2) for i, n in ahead]
-                nc.vector.tensor_add(out=sq[0][:], in0=sq[0][:], in1=sq[2][:])
-                sq_next += [clamp_and_square(i, n, 3) for i, n in ahead]
-                prod = terms.tile([P, B], F32, name="prod%d" % c)
+                sq_next = [clamp_and_square(ib_next, c_next, 0)]
+                add_pair(ib, c, sq, 0, whole)
+                sq_next.append(clamp_and_square(ib_next, c_next, 1))
+                add_pair(ib, c, sq, 2, whole)
+                sq_next.append(clamp_and_square(ib_next, c_next, 2))
+                add_halves(sq, whole)
+                sq_next.append(clamp_and_square(ib_next, c_next, 3))
+                prod = terms.tile([P, B], F32, name="term")
                 for ch in range(N_CHUNK):
-                    nc.vector.scalar_tensor_tensor(
-                        out=prod[:, chunks[ch]], in0=sq[0][:, chunks[ch]], scalar=offset[:, ib, c : c + 1],
-                        in1=sums[ch][:], op0=ALU.add, op1=ALU.mult,
-                    )
+                    multiply(ib, c, sq, sums, prod, ch)
                 term.append(prod)
                 if c == STORE_AT:
-                    for done_ib, banks in waiting:
-                        store(done_ib, banks)
+                    for q, o_ps in enumerate(waiting):
+                        store(ib - 1, q, o_ps)
                     waiting = []
-                full = term
-                if c == N_C - 1 and ib + 1 < N_IB:
-                    term = [base_term(ib + 1)]
-                for i, n in ahead:
-                    sums_next = mx_sums(i, n)
+                if c == BASE_AT:
+                    sums = mx_sums(ib, N_C)
+                    base = terms.tile([P, B], F32, name="term")
+                    for ch in range(N_CHUNK):
+                        nc.scalar.copy(out=base[:, chunks[ch]], in_=sums[ch][:])
+                    term.append(base)
+                sums_next = mx_sums(ib_next, c_next)
                 if c == N_C - 1:
-                    waiting = [(ib, add_terms(full))]
-            for done_ib, banks in waiting:
-                store(done_ib, banks)
+                    waiting = [add_terms(term, q) for q in range(N_CHUNK)]
+                    term = []
+            ib, c = units[last]
+            prod = terms.tile([P, B], F32, name="term")
+            term.append(prod)
+            for ch in range(N_CHUNK):
+                add_pair(ib, c, sq_next, 0, chunks[ch])
+                add_pair(ib, c, sq_next, 2, chunks[ch])
+                add_halves(sq_next, chunks[ch])
+                multiply(ib, c, sq_next, sums_next, prod, ch)
+                store(ib, ch, add_terms(term, ch))

@@ -28,9 +28,10 @@ N_CHUNK = B // CHUNK
 TB_PER_BANK = CHUNK // P
 UPWARD = (0, 2)
 LOAD_TB = 4
-BASE_AT = 3
-STORE_AT = 2
-SPARE_TERMS = 2
+BASE = N_C
+PLANES = (0, 1, 2, 3, BASE, 4, 5, 6, 7)
+COPY_OF = ("a", "a", "b", "b")
+AHEAD = 7
 
 FLOPS = 2 * B * OUT * IN * (N_C + 1)
 
@@ -58,6 +59,13 @@ def spline_tables(nc, tabs, kn):
 
     def per_piece(name):
         return tabs.tile([P, N_PIECE, N_IB, N_C], F32, name=name)
+
+    def per_knot(name):
+        return tabs.tile([P, N_IB, N_KNOTS], F32, name=name)
+
+    shift_at = {d: per_knot("shift_at%d" % d) for d in range(1, N_PIECE)}
+    for d in range(1, N_PIECE):
+        vec.memset(shift_at[d][:], 0.0)
 
     spans = (1, 2, 3)
     inv_span = {s: tabs.tile([P, N_IB, N_KNOTS - s], F32, name="inv_span%d" % s) for s in spans}
@@ -121,10 +129,6 @@ def spline_tables(nc, tabs, kn):
     for d in range(N_PIECE):
         vec.tensor_sub(out=bias[:, d], in0=bias[:, d], in1=knot(2))
 
-    lo = per_piece("lo")
-    hi = per_piece("hi")
-    vec.tensor_copy(out=lo[:, 0], in_=knot(0))
-    vec.tensor_copy(out=hi[:, N_PIECE - 1], in_=knot(N_PIECE))
     inner = range(1, N_PIECE)
     left = {d: table("left%d" % d) for d in inner}
     right = {d: table("right%d" % d) for d in inner}
@@ -147,12 +151,24 @@ def spline_tables(nc, tabs, kn):
         vec.tensor_sub(out=right[d][:], in0=right[d][:], in1=left[d][:])
     for d in inner:
         vec.tensor_mul(out=right[d][:], in0=right[d][:], in1=steep[d][:])
+
+    diff = per_knot("diff")
+    room = per_knot("room")
+    low = {"a": per_knot("low_a"), "b": per_knot("low_b")}
+    high = {"a": per_knot("high_a"), "b": per_knot("high_b")}
     for d in inner:
-        vec.tensor_scalar_max(out=left[d][:], in0=right[d][:], scalar1=0.0)
-        vec.tensor_scalar_min(out=right[d][:], in0=right[d][:], scalar1=0.0)
-    for d in inner:
-        vec.tensor_sub(out=lo[:, d], in0=knot(d), in1=left[d][:])
-        vec.tensor_add(out=hi[:, d - 1], in0=knot(d), in1=right[d][:])
+        vec.tensor_copy(out=shift_at[d][:, :, d : d + N_C], in_=right[d][:])
+    vec.tensor_scalar(out=room[:], in0=shift_at[1][:], scalar1=-1.0, scalar2=0.0, op0=ALU.mult, op1=ALU.max)
+    vec.tensor_sub(out=diff[:], in0=shift_at[3][:], in1=shift_at[2][:])
+    vec.scalar_tensor_tensor(out=room[:], in0=shift_at[2][:], scalar=-1.0, in1=room[:], op0=ALU.mult, op1=ALU.max)
+    vec.tensor_max(out=room[:], in0=room[:], in1=diff[:])
+    vec.tensor_sub(out=high["a"][:], in0=kn[:], in1=room[:])
+    vec.tensor_sub(out=low["a"][:], in0=high["a"][:], in1=shift_at[1][:])
+    vec.tensor_sub(out=low["b"][:], in0=high["a"][:], in1=shift_at[2][:])
+    vec.tensor_add(out=high["b"][:], in0=high["a"][:], in1=diff[:])
+    lo = per_piece("lo")
+    for d in range(N_PIECE):
+        vec.tensor_copy(out=lo[:, d], in_=low[COPY_OF[d]][:, :, d : d + N_C])
 
     offset = table("offset")
     held = per_piece("held")
@@ -177,7 +193,7 @@ def spline_tables(nc, tabs, kn):
         vec.tensor_scalar_mul(out=root[:, d], in0=root[:, d], scalar1=0.5)
     for d in UPWARD:
         vec.tensor_mul(out=root_bias[:, d], in0=root[:, d], in1=bias[:, d])
-    return gain, bias, lo, hi, offset, root, root_bias
+    return gain, bias, low, high, offset, root, root_bias
 
 
 def tile_kanlayer_t_kernel(tc, x, base_weight, spline_weight, grid, grad_out, out):
@@ -185,9 +201,7 @@ def tile_kanlayer_t_kernel(tc, x, base_weight, spline_weight, grid, grad_out, ou
     with ExitStack() as ctx:
         keep = ctx.enter_context(tc.tile_pool(name="keep", bufs=1))
         tabs = ctx.enter_context(tc.tile_pool(name="tabs", bufs=1))
-        clamped = ctx.enter_context(tc.tile_pool(name="clamped", bufs=5))
-        squares = ctx.enter_context(tc.tile_pool(name="squares", bufs=6))
-        rows = ctx.enter_context(tc.tile_pool(name="rows", bufs=2))
+        w_stage = ctx.enter_context(tc.tile_pool(name="w_stage", bufs=1))
         psum_c = ctx.enter_context(tc.psum_pool(name="psum_c", bufs=4))
         psum_t = ctx.enter_context(tc.psum_pool(name="psum_t", bufs=4))
 
@@ -197,10 +211,25 @@ def tile_kanlayer_t_kernel(tc, x, base_weight, spline_weight, grid, grad_out, ou
         make_identity(nc, ident_f[:])
 
         x_t = keep.tile([P, N_IB, B], BF16, name="x_t")
-        w_codes = keep.tile([P, N_C + 1, IN], U32, name="w_codes", align_bytes=64)
-        w_scales = keep.tile([P, N_C + 1, IN], U8, name="w_scales", align_bytes=64)
+        w_codes = keep.tile([P, N_IB, N_C * P], U32, name="w_codes", align_bytes=64)
+        w_scales = keep.tile([P, N_IB, N_C * P], U8, name="w_scales", align_bytes=64)
+        b_codes = keep.tile([P, IN], U32, name="b_codes", align_bytes=64)
+        b_scales = keep.tile([P, IN], U8, name="b_scales", align_bytes=64)
         g_codes = keep.tile([P, B], U32, name="g_codes", align_bytes=64)
         g_scales = keep.tile([P, B], U8, name="g_scales", align_bytes=64)
+
+        w_raws = [w_stage.tile([P, PACK, P * N_C], BF16, name="w_raw%d" % ib) for ib in range(N_IB)]
+        w_grps = [w_stage.tile([P, N_C, P, PACK], BF16, name="w_grp%d" % (ib % 2), align_bytes=64) for ib in range(2)]
+
+        def w_view(ib):
+            return w_raws[ib][:].rearrange("p j (i c) -> p c i j", c=N_C)
+
+        def w_quantize(ib):
+            nc.vector.quantize_mx(
+                out=w_codes[:, ib, :].bitcast(E4M3X4),
+                scales=w_scales[:, ib, :],
+                in_=w_grps[ib % 2][:].rearrange("p c i j -> p (c i j)"),
+            )
 
         with tc.tile_pool(name="load", bufs=1) as load, tc.tile_pool(name="stream", bufs=2) as stream:
             kn_bf = load.tile([P, N_IB, N_KNOTS], BF16, name="kn_bf")
@@ -217,15 +246,19 @@ def tile_kanlayer_t_kernel(tc, x, base_weight, spline_weight, grid, grad_out, ou
                 g_sb = load.tile([P, LOAD_TB, OUT], BF16, name="g_sb%d" % l)
                 nc.sync.dma_start(out=g_sb[:], in_=g_blocks[l])
                 g_sbs.append(g_sb)
-            w_raw = load.tile([P, PACK, IN * N_C], BF16, name="w_raw")
-            nc.sync.dma_start(out=w_raw[:], in_=spline_weight.rearrange("(p j) i c -> p j (i c)", j=PACK))
+            w_rows = spline_weight.rearrange("(p j) i c -> p j i c", j=PACK)
             b_raw = load.tile([P, PACK, IN], BF16, name="b_raw")
-            nc.sync.dma_start(out=b_raw[:], in_=base_weight.rearrange("(p j) i -> p j i", j=PACK))
+            for ib in range(N_IB):
+                nc.sync.dma_start(
+                    out=w_raws[ib][:].rearrange("p j (i c) -> p j i c", c=N_C), in_=w_rows[:, :, ib * P : (ib + 1) * P, :]
+                )
+                if ib == 0:
+                    nc.sync.dma_start(out=b_raw[:], in_=base_weight.rearrange("(p j) i -> p j i", j=PACK))
 
             kn = tabs.tile([P, N_IB, N_KNOTS], F32, name="kn")
             nc.vector.tensor_copy(out=kn[:], in_=kn_bf[:])
             with tc.manual_schedule():
-                gain, bias, lo, hi, offset, root, root_bias = spline_tables(nc, tabs, kn)
+                gain, bias, low, high, offset, root, root_bias = spline_tables(nc, tabs, kn)
 
             for ib in range(N_IB):
                 for half in range(2):
@@ -259,130 +292,132 @@ def tile_kanlayer_t_kernel(tc, x, base_weight, spline_weight, grid, grad_out, ou
                     in_=g_grp[:].rearrange("p k t -> p (k t)"),
                 )
 
-            w_by_c = w_raw[:].rearrange("p j (i c) -> p c i j", c=N_C)
-            for c in range(N_C + 1):
-                w_grp = stream.tile([P, IN, PACK], BF16, name="w_grp", align_bytes=64)
-                if c < N_C:
-                    nc.scalar.copy(out=w_grp[:], in_=w_by_c[:, c])
-                else:
-                    nc.scalar.copy(out=w_grp[:], in_=b_raw[:].rearrange("p j i -> p i j"))
-                nc.vector.quantize_mx(
-                    out=w_codes[:, c, :].bitcast(E4M3X4),
-                    scales=w_scales[:, c, :],
-                    in_=w_grp[:].rearrange("p i j -> p (i j)"),
-                )
+            nc.scalar.copy(out=w_grps[0][:], in_=w_view(0))
+            w_quantize(0)
+            b_grp = stream.tile([P, IN, PACK], BF16, name="b_grp", align_bytes=64)
+            nc.scalar.copy(out=b_grp[:], in_=b_raw[:].rearrange("p j i -> p i j"))
+            nc.vector.quantize_mx(
+                out=b_codes[:].bitcast(E4M3X4), scales=b_scales[:], in_=b_grp[:].rearrange("p i j -> p (i j)")
+            )
 
-        terms = ctx.enter_context(tc.tile_pool(name="terms", bufs=N_C + 1 + SPARE_TERMS))
+        clamped = ctx.enter_context(tc.tile_pool(name="clamped", bufs=4))
+        squares = ctx.enter_context(tc.tile_pool(name="squares", bufs=8))
+        prods = ctx.enter_context(tc.tile_pool(name="prods", bufs=8))
+        rows = ctx.enter_context(tc.tile_pool(name="rows", bufs=3))
         out_rows = out.rearrange("(q t p) f -> q p t f", t=TB_PER_BANK, p=P)
         chunks = [slice(ch * CHUNK, (ch + 1) * CHUNK) for ch in range(N_CHUNK)]
-        whole = slice(0, B)
+        copies = {}
 
-        def clamp_and_square(ib, c, d):
+        def clamp(ib, c):
+            for d in range(N_PIECE):
+                k = c + d
+                if (ib, k, COPY_OF[d]) not in copies:
+                    u = clamped.tile([P, B], BF16, name="u_" + COPY_OF[d])
+                    nc.gpsimd.tensor_scalar(
+                        out=u[:], in0=x_t[:, ib, :],
+                        scalar1=high[COPY_OF[d]][:, ib, k + 1 : k + 2], scalar2=low[COPY_OF[d]][:, ib, k : k + 1],
+                        op0=ALU.min, op1=ALU.max,
+                    )
+                    copies[(ib, k, COPY_OF[d])] = u
+
+        def square(ib, c, d):
             one = slice(c, c + 1)
-            u = clamped.tile([P, B], BF16, name="u")
-            nc.vector.tensor_scalar(
-                out=u[:], in0=x_t[:, ib, :], scalar1=lo[:, d, ib, one], scalar2=hi[:, d, ib, one],
-                op0=ALU.max, op1=ALU.min,
-            )
-            sq = squares.tile([P, B], F32, name="sq")
+            u = copies[(ib, c + d, COPY_OF[d])]
+            s = squares.tile([P, B], F32, name="sq")
             if d in UPWARD:
                 nc.scalar.activation(
-                    out=sq[:], in_=u[:], func=ACT.Square, bias=root_bias[:, d, ib, one], scale=root[:, d, ib, one]
+                    out=s[:], in_=u[:], func=ACT.Square, bias=root_bias[:, d, ib, one], scale=root[:, d, ib, one]
                 )
             else:
-                nc.scalar.activation(out=sq[:], in_=u[:], func=ACT.Square, bias=bias[:, d, ib, one], scale=1.0)
-            return sq
+                nc.scalar.activation(out=s[:], in_=u[:], func=ACT.Square, bias=bias[:, d, ib, one], scale=1.0)
+            return s
 
-        def add_pair(ib, c, sq, d, toks):
-            nc.vector.scalar_tensor_tensor(
-                out=sq[d][:, toks], in0=sq[d + 1][:, toks], scalar=gain[:, d + 1, ib, c : c + 1], in1=sq[d][:, toks],
-                op0=ALU.mult, op1=ALU.add,
+        def mx_sum(ib, plane, ch):
+            c_ps = psum_c.tile([P, CHUNK], F32, name="c_ps")
+            if plane == BASE:
+                codes, scales = b_codes[:, ib * P : (ib + 1) * P], b_scales[:, ib * P : (ib + 1) * P]
+            else:
+                codes, scales = w_codes[:, ib, plane * P : (plane + 1) * P], w_scales[:, ib, plane * P : (plane + 1) * P]
+            nc.tensor.matmul_mx(
+                out=c_ps[:],
+                lhsT=codes.bitcast(E4M3X4),
+                lhsT_scale=scales,
+                rhs=g_codes[:, chunks[ch]].bitcast(E5M2X4),
+                rhs_scale=g_scales[:, chunks[ch]],
+                start=True,
+                stop=True,
             )
+            return c_ps
 
-        def add_halves(sq, toks):
-            nc.vector.tensor_add(out=sq[0][:, toks], in0=sq[0][:, toks], in1=sq[2][:, toks])
-
-        def multiply(ib, c, sq, sums, prod, ch):
-            nc.vector.scalar_tensor_tensor(
-                out=prod[:, chunks[ch]], in0=sq[0][:, chunks[ch]], scalar=offset[:, ib, c : c + 1], in1=sums[ch][:],
-                op0=ALU.add, op1=ALU.mult,
-            )
-
-        def mx_sums(ib, c):
-            feats = slice(ib * P, (ib + 1) * P)
-            sums = []
-            for toks in chunks:
-                c_ps = psum_c.tile([P, CHUNK], F32, name="c_ps")
-                nc.tensor.matmul_mx(
-                    out=c_ps[:],
-                    lhsT=w_codes[:, c, feats].bitcast(E4M3X4),
-                    lhsT_scale=w_scales[:, c, feats],
-                    rhs=g_codes[:, toks].bitcast(E5M2X4),
-                    rhs_scale=g_scales[:, toks],
-                    start=True,
-                    stop=True,
-                )
-                sums.append(c_ps)
-            return sums
-
-        def add_terms(term, q):
-            o_ps = psum_t.tile([P, TB_PER_BANK, P], F32, name="o_ps", tag="bank")
+        def add_up(prod, bank, first, last):
             for t in range(TB_PER_BANK):
-                tb = q * TB_PER_BANK + t
-                for n in range(N_C + 1):
-                    nc.tensor.matmul(
-                        o_ps[:, t, :], lhsT=term[n][:, tb * P : (tb + 1) * P], rhs=ident_f[:],
-                        is_transpose=True, start=(n == 0), stop=(n == N_C),
-                    )
-            return o_ps
+                nc.tensor.matmul(
+                    bank[:, t, :], lhsT=prod[:, t * P : (t + 1) * P], rhs=ident_f[:], is_transpose=True,
+                    start=(first and t == 0), stop=(last and t == TB_PER_BANK - 1),
+                )
+
+        def term(ib, plane, d, s, c_ps, ch, bank):
+            prod = prods.tile([P, CHUNK], F32, name="prod")
+            one = slice(plane, plane + 1)
+            if plane == BASE:
+                nc.vector.tensor_copy(out=prod[:], in_=c_ps[:])
+            elif d == 0:
+                nc.vector.scalar_tensor_tensor(
+                    out=prod[:], in0=s[:, chunks[ch]], scalar=offset[:, ib, one], in1=c_ps[:], op0=ALU.add, op1=ALU.mult
+                )
+            elif d in UPWARD:
+                nc.vector.tensor_mul(out=prod[:], in0=s[:, chunks[ch]], in1=c_ps[:])
+            else:
+                nc.vector.scalar_tensor_tensor(
+                    out=prod[:], in0=s[:, chunks[ch]], scalar=gain[:, d, ib, one], in1=c_ps[:], op0=ALU.mult, op1=ALU.mult
+                )
+            add_up(prod, bank, plane == PLANES[0] and d == 0, plane == PLANES[-1] and d == N_PIECE - 1)
 
         def store(ib, q, o_ps):
             o_sb = rows.tile([P, TB_PER_BANK, P], F32, name="o_sb")
             nc.scalar.copy(out=o_sb[:], in_=o_ps[:])
             nc.sync.dma_start(out=out_rows[q][:, :, ib * P : (ib + 1) * P], in_=o_sb[:])
 
-        units = [(ib, c) for ib in range(N_IB) for c in range(N_C)]
-        last = len(units) - 1
+        steps = [(ib, plane) for ib in range(N_IB) for plane in PLANES]
+        bases = [(ib, c) for ib in range(N_IB) for c in range(N_C)]
+        made = {}
+
+        def square_ahead(m):
+            if m < N_PIECE * len(bases):
+                s, d = divmod(m, N_PIECE)
+                if d == 0 and s + 1 < len(bases):
+                    clamp(bases[s + 1][0], bases[s + 1][1])
+                made[m] = square(bases[s][0], bases[s][1], d)
+
         with tc.manual_schedule():
-            sq_next = [clamp_and_square(0, 0, d) for d in range(N_PIECE)]
-            sums_next = mx_sums(0, 0)
-            term = []
-            waiting = []
-            for k in range(last):
-                ib, c = units[k]
-                ib_next, c_next = units[k + 1]
-                sq, sums = sq_next, sums_next
-                sq_next = [clamp_and_square(ib_next, c_next, 0)]
-                add_pair(ib, c, sq, 0, whole)
-                sq_next.append(clamp_and_square(ib_next, c_next, 1))
-                add_pair(ib, c, sq, 2, whole)
-                sq_next.append(clamp_and_square(ib_next, c_next, 2))
-                add_halves(sq, whole)
-                sq_next.append(clamp_and_square(ib_next, c_next, 3))
-                prod = terms.tile([P, B], F32, name="term")
-                for ch in range(N_CHUNK):
-                    multiply(ib, c, sq, sums, prod, ch)
-                term.append(prod)
-                if c == STORE_AT:
-                    for q, o_ps in enumerate(waiting):
-                        store(ib - 1, q, o_ps)
-                    waiting = []
-                if c == BASE_AT:
-                    sums = mx_sums(ib, N_C)
-                    base = terms.tile([P, B], F32, name="term")
+            clamp(0, 0)
+            for m in range(AHEAD):
+                square_ahead(m)
+            sums_next = [mx_sum(0, PLANES[0], ch) for ch in range(N_CHUNK)]
+            banks = []
+            m = 0
+            for n in range(len(steps)):
+                ib, plane = steps[n]
+                sums, sums_next = sums_next, []
+                if plane == PLANES[0]:
+                    banks = [psum_t.tile([P, TB_PER_BANK, P], F32, name="o_ps", tag="bank") for ch in range(N_CHUNK)]
+                if plane == PLANES[1] and ib + 1 < N_IB:
+                    nc.gpsimd.tensor_scalar(
+                        out=w_grps[(ib + 1) % 2][:], in0=w_view(ib + 1), scalar1=1.0, scalar2=0.0, op0=ALU.mult, op1=ALU.add
+                    )
+                if plane == PLANES[5] and ib + 1 < N_IB:
+                    w_quantize(ib + 1)
+                for d in range(1 if plane == BASE else N_PIECE):
+                    closing = plane == BASE or d == N_PIECE - 1
+                    s = None
+                    if plane != BASE:
+                        square_ahead(m + AHEAD)
+                        s = made[m]
+                        m += 1
                     for ch in range(N_CHUNK):
-                        nc.scalar.copy(out=base[:, chunks[ch]], in_=sums[ch][:])
-                    term.append(base)
-                sums_next = mx_sums(ib_next, c_next)
-                if c == N_C - 1:
-                    waiting = [add_terms(term, q) for q in range(N_CHUNK)]
-                    term = []
-            ib, c = units[last]
-            prod = terms.tile([P, B], F32, name="term")
-            term.append(prod)
-            for ch in range(N_CHUNK):
-                add_pair(ib, c, sq_next, 0, chunks[ch])
-                add_pair(ib, c, sq_next, 2, chunks[ch])
-                add_halves(sq_next, chunks[ch])
-                multiply(ib, c, sq_next, sums_next, prod, ch)
-                store(ib, ch, add_terms(term, ch))
+                        term(ib, plane, d, s, sums[ch], ch, banks[ch])
+                        if closing and ch % 2 == 1 and n + 1 < len(steps):
+                            sums_next.append(mx_sum(steps[n + 1][0], steps[n + 1][1], ch - 1))
+                            sums_next.append(mx_sum(steps[n + 1][0], steps[n + 1][1], ch))
+                        if closing and plane == PLANES[-1]:
+                            store(ib, ch, banks[ch])

@@ -31,7 +31,7 @@ LOAD_TB = 4
 BASE = N_C
 PLANES = (0, 1, 2, 3, BASE, 4, 5, 6, 7)
 COPY_OF = ("a", "a", "b", "b")
-AHEAD = 7
+AHEAD = 4
 
 FLOPS = 2 * B * OUT * IN * (N_C + 1)
 
@@ -45,154 +45,137 @@ PATHS = (
     (2, 1, 2, 2, (4, 4, 2)),
     (3, 1, 2, 3, (4, 4, 4)),
 )
-SIGN = (1.0, -1.0, 1.0, -1.0)
 
 
-def spline_tables(nc, tabs, kn):
+def spline_tables(nc, tabs, kn_bf):
     vec = nc.vector
 
-    def knot(e):
-        return kn[:, :, e : e + N_C]
-
-    def table(name):
-        return tabs.tile([P, N_IB, N_C], F32, name=name)
-
-    def per_piece(name):
-        return tabs.tile([P, N_PIECE, N_IB, N_C], F32, name=name)
+    def stack(n, name):
+        return tabs.tile([P, n, N_IB, N_C], F32, name=name)
 
     def per_knot(name):
         return tabs.tile([P, N_IB, N_KNOTS], F32, name=name)
 
-    shift_at = {d: per_knot("shift_at%d" % d) for d in range(1, N_PIECE)}
-    for d in range(1, N_PIECE):
-        vec.memset(shift_at[d][:], 0.0)
+    def spread(ap, n):
+        return ap.to_broadcast([P, n, N_IB, N_C])
 
-    spans = (1, 2, 3)
-    inv_span = {s: tabs.tile([P, N_IB, N_KNOTS - s], F32, name="inv_span%d" % s) for s in spans}
-    for s in spans:
-        vec.tensor_sub(out=inv_span[s][:], in0=kn[:, :, s:N_KNOTS], in1=kn[:, :, 0 : N_KNOTS - s])
-    for s in spans:
-        vec.tensor_scalar_add(out=inv_span[s][:], in0=inv_span[s][:], scalar1=EPS)
-    for s in spans:
-        vec.reciprocal(out=inv_span[s][:], in_=inv_span[s][:])
+    shift_at = tabs.tile([P, N_PIECE - 1, N_IB, N_KNOTS], F32, name="shift_at")
+    vec.memset(shift_at[:], 0.0)
 
-    rel = [table("rel%d" % e) for e in range(5)]
+    tau = stack(5, "tau")
     for e in range(5):
-        vec.tensor_sub(out=rel[e][:], in0=knot(e), in1=knot(2))
+        vec.tensor_copy(out=tau[:, e], in_=kn_bf[:, :, e : e + N_C])
+    span = stack(9, "span")
+    inv = stack(9, "inv")
+    at = {1: 0, 2: 4, 3: 7}
+    for s in (3, 2, 1):
+        vec.scalar_tensor_tensor(
+            out=span[:, at[s] : at[s] + 5 - s], in0=tau[:, s:5], scalar=EPS, in1=tau[:, 0 : 5 - s],
+            op0=ALU.add, op1=ALU.subtract,
+        )
+    rel = stack(5, "rel")
+    vec.tensor_sub(out=rel[:], in0=tau[:], in1=spread(tau[:, 2:3], 5))
+    kn = per_knot("kn")
+    vec.tensor_copy(out=kn[:], in_=kn_bf[:])
+    vec.reciprocal(out=inv[:], in_=span[:])
 
-    n_paths = range(len(PATHS))
-    k = [table("k%d" % n) for n in n_paths]
-    pair = [table("pair%d" % n) for n in n_paths]
-    sum1 = [table("sum1_%d" % n) for n in n_paths]
-    sum2 = [table("sum2_%d" % n) for n in n_paths]
-    cross = [table("cross%d" % n) for n in n_paths]
-    for n, (d, e3, e2, e1, (a, b, c)) in enumerate(PATHS):
-        vec.tensor_mul(out=k[n][:], in0=inv_span[3][:, :, e3 : e3 + N_C], in1=inv_span[2][:, :, e2 : e2 + N_C])
-    for n, (d, e3, e2, e1, (a, b, c)) in enumerate(PATHS):
-        vec.tensor_add(out=pair[n][:], in0=rel[a][:], in1=rel[b][:])
-    for n, (d, e3, e2, e1, (a, b, c)) in enumerate(PATHS):
-        vec.tensor_mul(out=k[n][:], in0=k[n][:], in1=inv_span[1][:, :, e1 : e1 + N_C])
-    for n, (d, e3, e2, e1, (a, b, c)) in enumerate(PATHS):
-        vec.tensor_mul(out=sum2[n][:], in0=rel[a][:], in1=rel[b][:])
-    for n, (d, e3, e2, e1, (a, b, c)) in enumerate(PATHS):
-        vec.tensor_add(out=sum1[n][:], in0=pair[n][:], in1=rel[c][:])
-    for n, (d, e3, e2, e1, (a, b, c)) in enumerate(PATHS):
-        vec.tensor_mul(out=cross[n][:], in0=pair[n][:], in1=rel[c][:])
-    for n in n_paths:
-        vec.tensor_mul(out=sum1[n][:], in0=sum1[n][:], in1=k[n][:])
-    for n in n_paths:
-        vec.tensor_add(out=sum2[n][:], in0=sum2[n][:], in1=cross[n][:])
-    for n in n_paths:
-        vec.tensor_mul(out=sum2[n][:], in0=sum2[n][:], in1=k[n][:])
+    ends = rel[:, 0:5:4]
+    sum13 = stack(1, "sum13")
+    prod13 = stack(1, "prod13")
+    squared = stack(5, "squared")
+    twice = stack(2, "twice")
+    sym = tabs.tile([P, 2, len(PATHS), N_IB, N_C], F32, name="sym")
+    vec.tensor_add(out=sum13[:, 0], in0=rel[:, 1], in1=rel[:, 3])
+    vec.tensor_mul(out=squared[:], in0=rel[:], in1=rel[:])
+    vec.tensor_mul(out=prod13[:, 0], in0=rel[:, 1], in1=rel[:, 3])
+    pair = stack(4, "pair")
+    vec.scalar_tensor_tensor(
+        out=pair[:, 0:2], in0=inv[:, 4:6], scalar=3.0, in1=spread(inv[:, 7:8], 2), op0=ALU.mult, op1=ALU.mult
+    )
+    vec.scalar_tensor_tensor(
+        out=pair[:, 2:4], in0=inv[:, 5:7], scalar=3.0, in1=spread(inv[:, 8:9], 2), op0=ALU.mult, op1=ALU.mult
+    )
+    vec.tensor_scalar_mul(out=sym[:, 0, 0:8:7], in0=ends, scalar1=3.0)
+    vec.tensor_scalar_mul(out=sym[:, 0, 1:7:5], in0=ends, scalar1=2.0)
+    vec.tensor_add(out=sym[:, 0, 2:6:3], in0=ends, in1=spread(sum13[:], 2))
+    vec.scalar_tensor_tensor(out=sym[:, 0, 3], in0=rel[:, 1], scalar=2.0, in1=rel[:, 4], op0=ALU.mult, op1=ALU.add)
+    vec.scalar_tensor_tensor(out=sym[:, 0, 4], in0=rel[:, 3], scalar=2.0, in1=rel[:, 0], op0=ALU.mult, op1=ALU.add)
+    poly = tabs.tile([P, 3, len(PATHS), N_IB, N_C], F32, name="poly")
+    vec.tensor_mul(out=poly[:, 0, 0], in0=pair[:, 0], in1=inv[:, 0])
+    vec.scalar_tensor_tensor(
+        out=poly[:, 0, 1:4], in0=pair[:, 0:3], scalar=-1.0, in1=spread(inv[:, 1:2], 3), op0=ALU.mult, op1=ALU.mult
+    )
+    vec.tensor_mul(out=poly[:, 0, 4:7], in0=pair[:, 1:4], in1=spread(inv[:, 2:3], 3))
+    vec.scalar_tensor_tensor(out=poly[:, 0, 7], in0=pair[:, 3], scalar=-1.0, in1=inv[:, 3], op0=ALU.mult, op1=ALU.mult)
+    vec.scalar_tensor_tensor(out=twice[:, 0], in0=rel[:, 4], scalar=2.0, in1=rel[:, 1], op0=ALU.mult, op1=ALU.add)
+    vec.scalar_tensor_tensor(out=twice[:, 1], in0=rel[:, 0], scalar=2.0, in1=rel[:, 3], op0=ALU.mult, op1=ALU.add)
+    vec.tensor_scalar_mul(out=sym[:, 1, 0:8:7], in0=squared[:, 0:5:4], scalar1=3.0)
+    vec.tensor_copy(out=sym[:, 1, 1:7:5], in_=squared[:, 0:5:4])
+    vec.tensor_mul(out=sym[:, 1, 2:6:3], in0=ends, in1=spread(sum13[:], 2))
+    vec.tensor_mul(out=sym[:, 1, 3:5], in0=twice[:], in1=rel[:, 1:4:2])
+    vec.scalar_tensor_tensor(out=poly[:, 1], in0=poly[:, 0], scalar=-2.0 / 3.0, in1=sym[:, 0], op0=ALU.mult, op1=ALU.mult)
+    vec.tensor_add(out=sym[:, 1, 2:6:3], in0=sym[:, 1, 2:6:3], in1=spread(prod13[:], 2))
+    vec.scalar_tensor_tensor(out=poly[:, 2], in0=poly[:, 0], scalar=1.0 / 3.0, in1=sym[:, 1], op0=ALU.mult, op1=ALU.mult)
 
-    gain = per_piece("gain")
-    lin = per_piece("lin")
-    con = per_piece("con")
-    parts = ((gain, k, 3.0), (lin, sum1, -2.0), (con, sum2, 1.0))
-    first = [[p[0] for p in PATHS].index(d) for d in range(N_PIECE)]
-    for d in range(N_PIECE):
-        for total, part, factor in parts:
-            vec.tensor_scalar_mul(out=total[:, d], in0=part[first[d]][:], scalar1=factor * SIGN[d])
-    for n, path in enumerate(PATHS):
-        d = path[0]
-        if n != first[d]:
-            for total, part, factor in parts:
-                vec.scalar_tensor_tensor(
-                    out=total[:, d], in0=part[n][:], scalar=factor * SIGN[d], in1=total[:, d],
-                    op0=ALU.mult, op1=ALU.add,
-                )
+    quad = tabs.tile([P, 3, N_PIECE, N_IB, N_C], F32, name="quad")
+    vec.tensor_copy(out=quad[:, :, 0:4:3], in_=poly[:, :, 0:8:7])
+    vec.tensor_add(out=quad[:, :, 1:3], in0=poly[:, :, 1:5:3], in1=poly[:, :, 2:6:3])
+    vec.tensor_add(out=quad[:, :, 1:3], in0=quad[:, :, 1:3], in1=poly[:, :, 3:7:3])
+    gain, lin = quad[:, 0], quad[:, 1]
 
-    bias = per_piece("bias")
-    inv_gain = per_piece("inv_gain")
-    vec.reciprocal(out=inv_gain[:], in_=gain[:])
-    vec.scalar_tensor_tensor(out=bias[:], in0=lin[:], scalar=0.5, in1=inv_gain[:], op0=ALU.mult, op1=ALU.mult)
-    for d in range(N_PIECE):
-        vec.tensor_sub(out=bias[:, d], in0=bias[:, d], in1=knot(2))
+    root = stack(len(UPWARD), "root")
+    nc.scalar.sqrt(out=root[:], in_=gain[:, 0:3:2])
 
-    inner = range(1, N_PIECE)
-    left = {d: table("left%d" % d) for d in inner}
-    right = {d: table("right%d" % d) for d in inner}
-    steep = {d: table("steep%d" % d) for d in inner}
-    for d in inner:
-        vec.tensor_mul(out=left[d][:], in0=gain[:, d - 1], in1=rel[d][:])
-        vec.tensor_mul(out=right[d][:], in0=gain[:, d], in1=rel[d][:])
-    for d in inner:
-        vec.scalar_tensor_tensor(out=steep[d][:], in0=right[d][:], scalar=2.0, in1=lin[:, d], op0=ALU.mult, op1=ALU.add)
-        vec.tensor_add(out=left[d][:], in0=left[d][:], in1=lin[:, d - 1])
-        vec.tensor_add(out=right[d][:], in0=right[d][:], in1=lin[:, d])
-    for d in inner:
-        vec.reciprocal(out=steep[d][:], in_=steep[d][:])
-        vec.tensor_mul(out=left[d][:], in0=left[d][:], in1=rel[d][:])
-        vec.tensor_mul(out=right[d][:], in0=right[d][:], in1=rel[d][:])
-    for d in inner:
-        vec.tensor_add(out=left[d][:], in0=left[d][:], in1=con[:, d - 1])
-        vec.tensor_add(out=right[d][:], in0=right[d][:], in1=con[:, d])
-    for d in inner:
-        vec.tensor_sub(out=right[d][:], in0=right[d][:], in1=left[d][:])
-    for d in inner:
-        vec.tensor_mul(out=right[d][:], in0=right[d][:], in1=steep[d][:])
+    knots = rel[:, 1:4]
+    step = tabs.tile([P, 3, N_PIECE - 1, N_IB, N_C], F32, name="step")
+    jump = stack(3, "jump")
+    steep = stack(3, "steep")
+    inv_gain = stack(N_PIECE, "inv_gain")
+    bias = stack(N_PIECE, "bias")
+    vec.tensor_sub(out=step[:], in0=quad[:, :, 1:4], in1=quad[:, :, 0:3])
+    vec.tensor_mul(out=steep[:], in0=gain[:, 1:4], in1=knots)
+    vec.reciprocal(out=inv_gain[:], in_=gain)
+    vec.tensor_mul(out=jump[:], in0=step[:, 0], in1=knots)
+    vec.scalar_tensor_tensor(out=steep[:], in0=steep[:], scalar=2.0, in1=lin[:, 1:4], op0=ALU.mult, op1=ALU.add)
+    vec.scalar_tensor_tensor(out=bias[:], in0=lin, scalar=0.5, in1=inv_gain[:], op0=ALU.mult, op1=ALU.mult)
+    vec.tensor_add(out=jump[:], in0=jump[:], in1=step[:, 1])
+    vec.reciprocal(out=steep[:], in_=steep[:])
+    vec.tensor_sub(out=bias[:], in0=bias[:], in1=spread(tau[:, 2:3], N_PIECE))
+    vec.tensor_mul(out=jump[:], in0=jump[:], in1=knots)
+    vec.tensor_add(out=jump[:], in0=jump[:], in1=step[:, 2])
+    vec.tensor_mul(out=jump[:], in0=jump[:], in1=steep[:])
 
     diff = per_knot("diff")
     room = per_knot("room")
     low = {"a": per_knot("low_a"), "b": per_knot("low_b")}
     high = {"a": per_knot("high_a"), "b": per_knot("high_b")}
-    for d in inner:
-        vec.tensor_copy(out=shift_at[d][:, :, d : d + N_C], in_=right[d][:])
-    vec.tensor_scalar(out=room[:], in0=shift_at[1][:], scalar1=-1.0, scalar2=0.0, op0=ALU.mult, op1=ALU.max)
-    vec.tensor_sub(out=diff[:], in0=shift_at[3][:], in1=shift_at[2][:])
-    vec.scalar_tensor_tensor(out=room[:], in0=shift_at[2][:], scalar=-1.0, in1=room[:], op0=ALU.mult, op1=ALU.max)
+    for d in range(1, N_PIECE):
+        vec.tensor_copy(out=shift_at[:, d - 1, :, d : d + N_C], in_=jump[:, d - 1])
+    vec.tensor_scalar(out=room[:], in0=shift_at[:, 0], scalar1=-1.0, scalar2=0.0, op0=ALU.mult, op1=ALU.max)
+    vec.tensor_sub(out=diff[:], in0=shift_at[:, 2], in1=shift_at[:, 1])
+    vec.scalar_tensor_tensor(out=room[:], in0=shift_at[:, 1], scalar=-1.0, in1=room[:], op0=ALU.mult, op1=ALU.max)
     vec.tensor_max(out=room[:], in0=room[:], in1=diff[:])
     vec.tensor_sub(out=high["a"][:], in0=kn[:], in1=room[:])
-    vec.tensor_sub(out=low["a"][:], in0=high["a"][:], in1=shift_at[1][:])
-    vec.tensor_sub(out=low["b"][:], in0=high["a"][:], in1=shift_at[2][:])
+    vec.tensor_sub(out=low["a"][:], in0=high["a"][:], in1=shift_at[:, 0])
+    vec.tensor_sub(out=low["b"][:], in0=high["a"][:], in1=shift_at[:, 1])
     vec.tensor_add(out=high["b"][:], in0=high["a"][:], in1=diff[:])
-    lo = per_piece("lo")
+
+    ratio = stack(len(UPWARD), "ratio")
+    root_bias = stack(len(UPWARD), "root_bias")
+    vec.reciprocal(out=ratio[:], in_=root[:])
+    lo = stack(N_PIECE, "lo")
     for d in range(N_PIECE):
         vec.tensor_copy(out=lo[:, d], in_=low[COPY_OF[d]][:, :, d : d + N_C])
-
-    offset = table("offset")
-    held = per_piece("held")
-    vec.tensor_add(out=held[:], in0=lo[:], in1=bias[:])
-    vec.tensor_mul(out=held[:], in0=held[:], in1=held[:])
-    vec.scalar_tensor_tensor(out=held[:], in0=held[:], scalar=-1.0, in1=gain[:], op0=ALU.mult, op1=ALU.mult)
-    vec.tensor_add(out=offset[:], in0=held[:, 1], in1=held[:, 2])
-    vec.tensor_add(out=offset[:], in0=offset[:], in1=held[:, 3])
-
-    root = per_piece("root")
-    root_bias = per_piece("root_bias")
-    ratio = per_piece("ratio")
-    for d in UPWARD:
-        nc.scalar.sqrt(out=root[:, d], in_=gain[:, d])
-    for d in UPWARD:
-        vec.reciprocal(out=ratio[:, d], in_=root[:, d])
-    for d in UPWARD:
-        vec.tensor_mul(out=ratio[:, d], in0=ratio[:, d], in1=gain[:, d])
-    for d in UPWARD:
-        vec.tensor_add(out=root[:, d], in0=root[:, d], in1=ratio[:, d])
-    for d in UPWARD:
-        vec.tensor_scalar_mul(out=root[:, d], in0=root[:, d], scalar1=0.5)
-    for d in UPWARD:
-        vec.tensor_mul(out=root_bias[:, d], in0=root[:, d], in1=bias[:, d])
+    vec.tensor_mul(out=ratio[:], in0=ratio[:], in1=gain[:, 0:3:2])
+    vec.tensor_add(out=lo[:], in0=lo[:], in1=bias[:])
+    vec.tensor_add(out=root[:], in0=root[:], in1=ratio[:])
+    vec.tensor_mul(out=lo[:], in0=lo[:], in1=lo[:])
+    vec.tensor_scalar_mul(out=root[:], in0=root[:], scalar1=0.5)
+    offset = stack(1, "offset")
+    vec.scalar_tensor_tensor(out=lo[:], in0=lo[:], scalar=-1.0, in1=gain, op0=ALU.mult, op1=ALU.mult)
+    vec.tensor_mul(out=root_bias[:], in0=root[:], in1=bias[:, 0:3:2])
+    vec.tensor_add(out=offset[:, 0], in0=lo[:, 1], in1=lo[:, 2])
+    vec.tensor_add(out=offset[:, 0], in0=offset[:, 0], in1=lo[:, 3])
     return gain, bias, low, high, offset, root, root_bias
 
 
@@ -218,17 +201,25 @@ def tile_kanlayer_t_kernel(tc, x, base_weight, spline_weight, grid, grad_out, ou
         g_codes = keep.tile([P, B], U32, name="g_codes", align_bytes=64)
         g_scales = keep.tile([P, B], U8, name="g_scales", align_bytes=64)
 
-        w_raws = [w_stage.tile([P, PACK, P * N_C], BF16, name="w_raw%d" % ib) for ib in range(N_IB)]
-        w_grps = [w_stage.tile([P, N_C, P, PACK], BF16, name="w_grp%d" % (ib % 2), align_bytes=64) for ib in range(2)]
+        w_raws = [w_stage.tile([P, PACK, P * N_C], BF16, name="w_raw%d" % n) for n in range(2)]
+        w_grp = w_stage.tile([P, N_C, P, PACK], BF16, name="w_grp", align_bytes=64)
+        w_rows = spline_weight.rearrange("(p j) i c -> p j i c", j=PACK)
+        clamped = ctx.enter_context(tc.tile_pool(name="clamped", bufs=4))
+        squares = ctx.enter_context(tc.tile_pool(name="squares", bufs=8))
+
+        def w_load(ib):
+            nc.sync.dma_start(
+                out=w_raws[ib % 2][:].rearrange("p j (i c) -> p j i c", c=N_C), in_=w_rows[:, :, ib * P : (ib + 1) * P, :]
+            )
 
         def w_view(ib):
-            return w_raws[ib][:].rearrange("p j (i c) -> p c i j", c=N_C)
+            return w_raws[ib % 2][:].rearrange("p j (i c) -> p c i j", c=N_C)
 
         def w_quantize(ib):
             nc.vector.quantize_mx(
                 out=w_codes[:, ib, :].bitcast(E4M3X4),
                 scales=w_scales[:, ib, :],
-                in_=w_grps[ib % 2][:].rearrange("p c i j -> p (c i j)"),
+                in_=w_grp[:].rearrange("p c i j -> p (c i j)"),
             )
 
         with tc.tile_pool(name="load", bufs=1) as load, tc.tile_pool(name="stream", bufs=2) as stream:
@@ -246,19 +237,13 @@ def tile_kanlayer_t_kernel(tc, x, base_weight, spline_weight, grid, grad_out, ou
                 g_sb = load.tile([P, LOAD_TB, OUT], BF16, name="g_sb%d" % l)
                 nc.sync.dma_start(out=g_sb[:], in_=g_blocks[l])
                 g_sbs.append(g_sb)
-            w_rows = spline_weight.rearrange("(p j) i c -> p j i c", j=PACK)
             b_raw = load.tile([P, PACK, IN], BF16, name="b_raw")
-            for ib in range(N_IB):
-                nc.sync.dma_start(
-                    out=w_raws[ib][:].rearrange("p j (i c) -> p j i c", c=N_C), in_=w_rows[:, :, ib * P : (ib + 1) * P, :]
-                )
-                if ib == 0:
-                    nc.sync.dma_start(out=b_raw[:], in_=base_weight.rearrange("(p j) i -> p j i", j=PACK))
+            w_load(0)
+            nc.sync.dma_start(out=b_raw[:], in_=base_weight.rearrange("(p j) i -> p j i", j=PACK))
+            w_load(1)
 
-            kn = tabs.tile([P, N_IB, N_KNOTS], F32, name="kn")
-            nc.vector.tensor_copy(out=kn[:], in_=kn_bf[:])
             with tc.manual_schedule():
-                gain, bias, low, high, offset, root, root_bias = spline_tables(nc, tabs, kn)
+                gain, bias, low, high, offset, root, root_bias = spline_tables(nc, tabs, kn_bf)
 
             for ib in range(N_IB):
                 for half in range(2):
@@ -292,16 +277,14 @@ def tile_kanlayer_t_kernel(tc, x, base_weight, spline_weight, grid, grad_out, ou
                     in_=g_grp[:].rearrange("p k t -> p (k t)"),
                 )
 
-            nc.scalar.copy(out=w_grps[0][:], in_=w_view(0))
+            nc.scalar.copy(out=w_grp[:], in_=w_view(0))
             w_quantize(0)
-            b_grp = stream.tile([P, IN, PACK], BF16, name="b_grp", align_bytes=64)
+            b_grp = load.tile([P, IN, PACK], BF16, name="b_grp", align_bytes=64)
             nc.scalar.copy(out=b_grp[:], in_=b_raw[:].rearrange("p j i -> p i j"))
             nc.vector.quantize_mx(
                 out=b_codes[:].bitcast(E4M3X4), scales=b_scales[:], in_=b_grp[:].rearrange("p i j -> p (i j)")
             )
 
-        clamped = ctx.enter_context(tc.tile_pool(name="clamped", bufs=4))
-        squares = ctx.enter_context(tc.tile_pool(name="squares", bufs=8))
         prods = ctx.enter_context(tc.tile_pool(name="prods", bufs=8))
         rows = ctx.enter_context(tc.tile_pool(name="rows", bufs=3))
         out_rows = out.rearrange("(q t p) f -> q p t f", t=TB_PER_BANK, p=P)
@@ -326,7 +309,8 @@ def tile_kanlayer_t_kernel(tc, x, base_weight, spline_weight, grid, grad_out, ou
             s = squares.tile([P, B], F32, name="sq")
             if d in UPWARD:
                 nc.scalar.activation(
-                    out=s[:], in_=u[:], func=ACT.Square, bias=root_bias[:, d, ib, one], scale=root[:, d, ib, one]
+                    out=s[:], in_=u[:], func=ACT.Square,
+                    bias=root_bias[:, UPWARD.index(d), ib, one], scale=root[:, UPWARD.index(d), ib, one],
                 )
             else:
                 nc.scalar.activation(out=s[:], in_=u[:], func=ACT.Square, bias=bias[:, d, ib, one], scale=1.0)
@@ -363,7 +347,7 @@ def tile_kanlayer_t_kernel(tc, x, base_weight, spline_weight, grid, grad_out, ou
                 nc.vector.tensor_copy(out=prod[:], in_=c_ps[:])
             elif d == 0:
                 nc.vector.scalar_tensor_tensor(
-                    out=prod[:], in0=s[:, chunks[ch]], scalar=offset[:, ib, one], in1=c_ps[:], op0=ALU.add, op1=ALU.mult
+                    out=prod[:], in0=s[:, chunks[ch]], scalar=offset[:, 0, ib, one], in1=c_ps[:], op0=ALU.add, op1=ALU.mult
                 )
             elif d in UPWARD:
                 nc.vector.tensor_mul(out=prod[:], in0=s[:, chunks[ch]], in1=c_ps[:])
@@ -378,46 +362,45 @@ def tile_kanlayer_t_kernel(tc, x, base_weight, spline_weight, grid, grad_out, ou
             nc.scalar.copy(out=o_sb[:], in_=o_ps[:])
             nc.sync.dma_start(out=out_rows[q][:, :, ib * P : (ib + 1) * P], in_=o_sb[:])
 
-        steps = [(ib, plane) for ib in range(N_IB) for plane in PLANES]
-        bases = [(ib, c) for ib in range(N_IB) for c in range(N_C)]
+        jobs = [
+            (ib, plane, d) for ib in range(N_IB) for plane in PLANES for d in range(1 if plane == BASE else N_PIECE)
+        ]
         made = {}
 
-        def square_ahead(m):
-            if m < N_PIECE * len(bases):
-                s, d = divmod(m, N_PIECE)
-                if d == 0 and s + 1 < len(bases):
-                    clamp(bases[s + 1][0], bases[s + 1][1])
-                made[m] = square(bases[s][0], bases[s][1], d)
+        def square_ahead(q):
+            if q < len(jobs) and jobs[q][1] != BASE:
+                ib, c, d = jobs[q]
+                after = (ib, c + 1) if c + 1 < N_C else (ib + 1, 0)
+                if d == 0 and after[0] < N_IB:
+                    clamp(after[0], after[1])
+                made[q] = square(ib, c, d)
 
         with tc.manual_schedule():
             clamp(0, 0)
-            for m in range(AHEAD):
-                square_ahead(m)
-            sums_next = [mx_sum(0, PLANES[0], ch) for ch in range(N_CHUNK)]
-            banks = []
-            m = 0
-            for n in range(len(steps)):
-                ib, plane = steps[n]
-                sums, sums_next = sums_next, []
-                if plane == PLANES[0]:
-                    banks = [psum_t.tile([P, TB_PER_BANK, P], F32, name="o_ps", tag="bank") for ch in range(N_CHUNK)]
-                if plane == PLANES[1] and ib + 1 < N_IB:
-                    nc.gpsimd.tensor_scalar(
-                        out=w_grps[(ib + 1) % 2][:], in0=w_view(ib + 1), scalar1=1.0, scalar2=0.0, op0=ALU.mult, op1=ALU.add
-                    )
-                if plane == PLANES[5] and ib + 1 < N_IB:
-                    w_quantize(ib + 1)
-                for d in range(1 if plane == BASE else N_PIECE):
-                    closing = plane == BASE or d == N_PIECE - 1
-                    s = None
-                    if plane != BASE:
-                        square_ahead(m + AHEAD)
-                        s = made[m]
-                        m += 1
-                    for ch in range(N_CHUNK):
-                        term(ib, plane, d, s, sums[ch], ch, banks[ch])
-                        if closing and ch % 2 == 1 and n + 1 < len(steps):
-                            sums_next.append(mx_sum(steps[n + 1][0], steps[n + 1][1], ch - 1))
-                            sums_next.append(mx_sum(steps[n + 1][0], steps[n + 1][1], ch))
-                        if closing and plane == PLANES[-1]:
+            for q in range(AHEAD):
+                square_ahead(q)
+            sums = [mx_sum(0, PLANES[0], ch) for ch in range(N_CHUNK)]
+            banks = [None] * N_CHUNK
+            for r in range(len(jobs) + N_CHUNK - 1):
+                square_ahead(r + AHEAD)
+                if r < len(jobs):
+                    ib, plane, d = jobs[r]
+                    if d == 0 and plane == PLANES[1] and ib + 1 < N_IB:
+                        nc.gpsimd.tensor_scalar(
+                            out=w_grp[:], in0=w_view(ib + 1), scalar1=1.0, scalar2=0.0, op0=ALU.mult, op1=ALU.add
+                        )
+                    if d == 0 and plane == PLANES[2] and ib + 2 < N_IB:
+                        w_load(ib + 2)
+                    if d == 0 and plane == PLANES[5] and ib + 1 < N_IB:
+                        w_quantize(ib + 1)
+                for ch in range(N_CHUNK):
+                    q = r - ch
+                    if 0 <= q < len(jobs):
+                        ib, plane, d = jobs[q]
+                        if plane == PLANES[0] and d == 0:
+                            banks[ch] = psum_t.tile([P, TB_PER_BANK, P], F32, name="o_ps", tag="bank")
+                        term(ib, plane, d, made.get(q), sums[ch], ch, banks[ch])
+                        if q + 1 < len(jobs) and jobs[q + 1][1] != plane:
+                            sums[ch] = mx_sum(jobs[q + 1][0], jobs[q + 1][1], ch)
+                        if plane == PLANES[-1] and d == N_PIECE - 1:
                             store(ib, ch, banks[ch])

@@ -31,7 +31,8 @@ LOAD_TB = 4
 BASE = N_C
 PLANES = (0, 1, 2, 3, BASE, 4, 5, 6, 7)
 COPY_OF = ("a", "a", "b", "b")
-AHEAD = 4
+PAIRS = ((0, 2), (1, 3))
+AHEAD = 2
 
 FLOPS = 2 * B * OUT * IN * (N_C + 1)
 
@@ -123,8 +124,10 @@ def spline_tables(nc, tabs, kn_bf):
     vec.tensor_add(out=quad[:, :, 1:3], in0=quad[:, :, 1:3], in1=poly[:, :, 3:7:3])
     gain, lin = quad[:, 0], quad[:, 1]
 
-    root = stack(len(UPWARD), "root")
-    nc.scalar.sqrt(out=root[:], in_=gain[:, 0:3:2])
+    size = stack(N_PIECE, "size")
+    root = stack(N_PIECE, "root")
+    vec.scalar_tensor_tensor(out=size[:], in0=gain, scalar=-1.0, in1=gain, op0=ALU.mult, op1=ALU.max)
+    nc.scalar.sqrt(out=root[:], in_=size[:])
 
     knots = rel[:, 1:4]
     step = tabs.tile([P, 3, N_PIECE - 1, N_IB, N_C], F32, name="step")
@@ -160,23 +163,24 @@ def spline_tables(nc, tabs, kn_bf):
     vec.tensor_sub(out=low["b"][:], in0=high["a"][:], in1=shift_at[:, 1])
     vec.tensor_add(out=high["b"][:], in0=high["a"][:], in1=diff[:])
 
-    ratio = stack(len(UPWARD), "ratio")
-    root_bias = stack(len(UPWARD), "root_bias")
+    ratio = stack(N_PIECE, "ratio")
+    root_bias = stack(N_PIECE, "root_bias")
     vec.reciprocal(out=ratio[:], in_=root[:])
     lo = stack(N_PIECE, "lo")
     for d in range(N_PIECE):
         vec.tensor_copy(out=lo[:, d], in_=low[COPY_OF[d]][:, :, d : d + N_C])
-    vec.tensor_mul(out=ratio[:], in0=ratio[:], in1=gain[:, 0:3:2])
+    vec.tensor_mul(out=ratio[:], in0=ratio[:], in1=size[:])
     vec.tensor_add(out=lo[:], in0=lo[:], in1=bias[:])
     vec.tensor_add(out=root[:], in0=root[:], in1=ratio[:])
     vec.tensor_mul(out=lo[:], in0=lo[:], in1=lo[:])
     vec.tensor_scalar_mul(out=root[:], in0=root[:], scalar1=0.5)
     offset = stack(1, "offset")
     vec.scalar_tensor_tensor(out=lo[:], in0=lo[:], scalar=-1.0, in1=gain, op0=ALU.mult, op1=ALU.mult)
-    vec.tensor_mul(out=root_bias[:], in0=root[:], in1=bias[:, 0:3:2])
+    vec.tensor_mul(out=root_bias[:], in0=root[:], in1=bias[:])
     vec.tensor_add(out=offset[:, 0], in0=lo[:, 1], in1=lo[:, 2])
     vec.tensor_add(out=offset[:, 0], in0=offset[:, 0], in1=lo[:, 3])
-    return gain, bias, low, high, offset, root, root_bias
+    vec.tensor_scalar_mul(out=offset[:, 0], in0=offset[:, 0], scalar1=0.5)
+    return low, high, offset, root, root_bias
 
 
 def tile_kanlayer_t_kernel(tc, x, base_weight, spline_weight, grid, grad_out, out):
@@ -185,7 +189,7 @@ def tile_kanlayer_t_kernel(tc, x, base_weight, spline_weight, grid, grad_out, ou
         keep = ctx.enter_context(tc.tile_pool(name="keep", bufs=1))
         tabs = ctx.enter_context(tc.tile_pool(name="tabs", bufs=1))
         w_stage = ctx.enter_context(tc.tile_pool(name="w_stage", bufs=1))
-        psum_c = ctx.enter_context(tc.psum_pool(name="psum_c", bufs=4))
+        psum_c = ctx.enter_context(tc.psum_pool(name="psum_c", bufs=1))
         psum_t = ctx.enter_context(tc.psum_pool(name="psum_t", bufs=4))
 
         ident_bf = keep.tile([P, P], BF16, name="ident_bf")
@@ -205,7 +209,7 @@ def tile_kanlayer_t_kernel(tc, x, base_weight, spline_weight, grid, grad_out, ou
         w_grp = w_stage.tile([P, N_C, P, PACK], BF16, name="w_grp", align_bytes=64)
         w_rows = spline_weight.rearrange("(p j) i c -> p j i c", j=PACK)
         clamped = ctx.enter_context(tc.tile_pool(name="clamped", bufs=4))
-        squares = ctx.enter_context(tc.tile_pool(name="squares", bufs=8))
+        squares = ctx.enter_context(tc.tile_pool(name="squares", bufs=4))
 
         def w_load(ib):
             nc.sync.dma_start(
@@ -243,7 +247,7 @@ def tile_kanlayer_t_kernel(tc, x, base_weight, spline_weight, grid, grad_out, ou
             w_load(1)
 
             with tc.manual_schedule():
-                gain, bias, low, high, offset, root, root_bias = spline_tables(nc, tabs, kn_bf)
+                low, high, offset, root, root_bias = spline_tables(nc, tabs, kn_bf)
 
             for ib in range(N_IB):
                 for half in range(2):
@@ -285,7 +289,7 @@ def tile_kanlayer_t_kernel(tc, x, base_weight, spline_weight, grid, grad_out, ou
                 out=b_codes[:].bitcast(E4M3X4), scales=b_scales[:], in_=b_grp[:].rearrange("p i j -> p (i j)")
             )
 
-        prods = ctx.enter_context(tc.tile_pool(name="prods", bufs=8))
+        prods = ctx.enter_context(tc.tile_pool(name="prods", bufs=6))
         rows = ctx.enter_context(tc.tile_pool(name="rows", bufs=3))
         out_rows = out.rearrange("(q t p) f -> q p t f", t=TB_PER_BANK, p=P)
         chunks = [slice(ch * CHUNK, (ch + 1) * CHUNK) for ch in range(N_CHUNK)]
@@ -303,21 +307,18 @@ def tile_kanlayer_t_kernel(tc, x, base_weight, spline_weight, grid, grad_out, ou
                     )
                     copies[(ib, k, COPY_OF[d])] = u
 
-        def square(ib, c, d):
+        def square(ib, c, pair):
             one = slice(c, c + 1)
-            u = copies[(ib, c + d, COPY_OF[d])]
-            s = squares.tile([P, B], F32, name="sq")
-            if d in UPWARD:
+            s = squares.tile([P, 2, B], F32, name="sq")
+            for n, d in enumerate(PAIRS[pair]):
                 nc.scalar.activation(
-                    out=s[:], in_=u[:], func=ACT.Square,
-                    bias=root_bias[:, UPWARD.index(d), ib, one], scale=root[:, UPWARD.index(d), ib, one],
+                    out=s[:, n, :], in_=copies[(ib, c + d, COPY_OF[d])][:], func=ACT.Square,
+                    bias=root_bias[:, d, ib, one], scale=root[:, d, ib, one],
                 )
-            else:
-                nc.scalar.activation(out=s[:], in_=u[:], func=ACT.Square, bias=bias[:, d, ib, one], scale=1.0)
             return s
 
         def mx_sum(ib, plane, ch):
-            c_ps = psum_c.tile([P, CHUNK], F32, name="c_ps")
+            c_ps = psum_c.tile([P, CHUNK], F32, name="c_ps%d" % ch)
             if plane == BASE:
                 codes, scales = b_codes[:, ib * P : (ib + 1) * P], b_scales[:, ib * P : (ib + 1) * P]
             else:
@@ -340,40 +341,44 @@ def tile_kanlayer_t_kernel(tc, x, base_weight, spline_weight, grid, grad_out, ou
                     start=(first and t == 0), stop=(last and t == TB_PER_BANK - 1),
                 )
 
-        def term(ib, plane, d, s, c_ps, ch, bank):
-            prod = prods.tile([P, CHUNK], F32, name="prod")
-            one = slice(plane, plane + 1)
+        def term(ib, plane, pair, s, c_ps, ch, bank):
             if plane == BASE:
-                nc.vector.tensor_copy(out=prod[:], in_=c_ps[:])
-            elif d == 0:
+                prod = prods.tile([P, 2, CHUNK], F32, name="prod")
+                nc.vector.tensor_copy(out=prod[:, 0, :], in_=c_ps[:])
+                add_up(prod[:, 0, :], bank, False, False)
+                return
+            prod = prods.tile([P, 2, CHUNK], F32, name="prod")
+            twice = c_ps[:].unsqueeze(1).to_broadcast([P, 2, CHUNK])
+            if pair == 0:
                 nc.vector.scalar_tensor_tensor(
-                    out=prod[:], in0=s[:, chunks[ch]], scalar=offset[:, 0, ib, one], in1=c_ps[:], op0=ALU.add, op1=ALU.mult
+                    out=prod[:], in0=s[:, :, chunks[ch]], scalar=offset[:, 0, ib, plane : plane + 1], in1=twice,
+                    op0=ALU.add, op1=ALU.mult,
                 )
-            elif d in UPWARD:
-                nc.vector.tensor_mul(out=prod[:], in0=s[:, chunks[ch]], in1=c_ps[:])
             else:
                 nc.vector.scalar_tensor_tensor(
-                    out=prod[:], in0=s[:, chunks[ch]], scalar=gain[:, d, ib, one], in1=c_ps[:], op0=ALU.mult, op1=ALU.mult
+                    out=prod[:], in0=s[:, :, chunks[ch]], scalar=-1.0, in1=twice, op0=ALU.mult, op1=ALU.mult
                 )
-            add_up(prod, bank, plane == PLANES[0] and d == 0, plane == PLANES[-1] and d == N_PIECE - 1)
+            for n in range(2):
+                add_up(
+                    prod[:, n, :], bank, plane == PLANES[0] and pair == 0 and n == 0,
+                    plane == PLANES[-1] and pair == 1 and n == 1,
+                )
 
         def store(ib, q, o_ps):
             o_sb = rows.tile([P, TB_PER_BANK, P], F32, name="o_sb")
             nc.scalar.copy(out=o_sb[:], in_=o_ps[:])
             nc.sync.dma_start(out=out_rows[q][:, :, ib * P : (ib + 1) * P], in_=o_sb[:])
 
-        jobs = [
-            (ib, plane, d) for ib in range(N_IB) for plane in PLANES for d in range(1 if plane == BASE else N_PIECE)
-        ]
+        jobs = [(ib, plane, pair) for ib in range(N_IB) for plane in PLANES for pair in range(1 if plane == BASE else 2)]
         made = {}
 
         def square_ahead(q):
             if q < len(jobs) and jobs[q][1] != BASE:
-                ib, c, d = jobs[q]
+                ib, c, pair = jobs[q]
                 after = (ib, c + 1) if c + 1 < N_C else (ib + 1, 0)
-                if d == 0 and after[0] < N_IB:
+                if pair == 0 and after[0] < N_IB:
                     clamp(after[0], after[1])
-                made[q] = square(ib, c, d)
+                made[q] = square(ib, c, pair)
 
         with tc.manual_schedule():
             clamp(0, 0)
@@ -381,26 +386,26 @@ def tile_kanlayer_t_kernel(tc, x, base_weight, spline_weight, grid, grad_out, ou
                 square_ahead(q)
             sums = [mx_sum(0, PLANES[0], ch) for ch in range(N_CHUNK)]
             banks = [None] * N_CHUNK
-            for r in range(len(jobs) + N_CHUNK - 1):
+            for r in range(len(jobs) + 1):
                 square_ahead(r + AHEAD)
                 if r < len(jobs):
-                    ib, plane, d = jobs[r]
-                    if d == 0 and plane == PLANES[1] and ib + 1 < N_IB:
+                    ib, plane, pair = jobs[r]
+                    if pair == 0 and plane == PLANES[1] and ib + 1 < N_IB:
                         nc.gpsimd.tensor_scalar(
                             out=w_grp[:], in0=w_view(ib + 1), scalar1=1.0, scalar2=0.0, op0=ALU.mult, op1=ALU.add
                         )
-                    if d == 0 and plane == PLANES[2] and ib + 2 < N_IB:
+                    if pair == 0 and plane == PLANES[2] and ib + 2 < N_IB:
                         w_load(ib + 2)
-                    if d == 0 and plane == PLANES[5] and ib + 1 < N_IB:
+                    if pair == 0 and plane == PLANES[5] and ib + 1 < N_IB:
                         w_quantize(ib + 1)
                 for ch in range(N_CHUNK):
-                    q = r - ch
+                    q = r - ch // 2
                     if 0 <= q < len(jobs):
-                        ib, plane, d = jobs[q]
-                        if plane == PLANES[0] and d == 0:
+                        ib, plane, pair = jobs[q]
+                        if plane == PLANES[0] and pair == 0:
                             banks[ch] = psum_t.tile([P, TB_PER_BANK, P], F32, name="o_ps", tag="bank")
-                        term(ib, plane, d, made.get(q), sums[ch], ch, banks[ch])
+                        term(ib, plane, pair, made.get(q), sums[ch], ch, banks[ch])
                         if q + 1 < len(jobs) and jobs[q + 1][1] != plane:
                             sums[ch] = mx_sum(jobs[q + 1][0], jobs[q + 1][1], ch)
-                        if plane == PLANES[-1] and d == N_PIECE - 1:
+                        if plane == PLANES[-1] and pair == 1:
                             store(ib, ch, banks[ch])

@@ -33,6 +33,7 @@ PLANES = (0, 1, 2, 3, BASE, 4, 5, 6, 7)
 COPY_OF = ("a", "a", "b", "b")
 PAIRS = ((0, 2), (1, 3))
 AHEAD = 2
+LAG = 2
 
 FLOPS = 2 * B * OUT * IN * (N_C + 1)
 
@@ -289,7 +290,7 @@ def tile_kanlayer_t_kernel(tc, x, base_weight, spline_weight, grid, grad_out, ou
                 out=b_codes[:].bitcast(E4M3X4), scales=b_scales[:], in_=b_grp[:].rearrange("p i j -> p (i j)")
             )
 
-        prods = ctx.enter_context(tc.tile_pool(name="prods", bufs=6))
+        prods = ctx.enter_context(tc.tile_pool(name="prods", bufs=8))
         rows = ctx.enter_context(tc.tile_pool(name="rows", bufs=3))
         out_rows = out.rearrange("(q t p) f -> q p t f", t=TB_PER_BANK, p=P)
         chunks = [slice(ch * CHUNK, (ch + 1) * CHUNK) for ch in range(N_CHUNK)]
@@ -341,12 +342,11 @@ def tile_kanlayer_t_kernel(tc, x, base_weight, spline_weight, grid, grad_out, ou
                     start=(first and t == 0), stop=(last and t == TB_PER_BANK - 1),
                 )
 
-        def term(ib, plane, pair, s, c_ps, ch, bank):
+        def term(ib, plane, pair, s, c_ps, ch):
             if plane == BASE:
                 prod = prods.tile([P, 2, CHUNK], F32, name="prod")
                 nc.vector.tensor_copy(out=prod[:, 0, :], in_=c_ps[:])
-                add_up(prod[:, 0, :], bank, False, False)
-                return
+                return [(prod[:, 0, :], False, False)]
             prod = prods.tile([P, 2, CHUNK], F32, name="prod")
             twice = c_ps[:].unsqueeze(1).to_broadcast([P, 2, CHUNK])
             if pair == 0:
@@ -358,11 +358,10 @@ def tile_kanlayer_t_kernel(tc, x, base_weight, spline_weight, grid, grad_out, ou
                 nc.vector.scalar_tensor_tensor(
                     out=prod[:], in0=s[:, :, chunks[ch]], scalar=-1.0, in1=twice, op0=ALU.mult, op1=ALU.mult
                 )
-            for n in range(2):
-                add_up(
-                    prod[:, n, :], bank, plane == PLANES[0] and pair == 0 and n == 0,
-                    plane == PLANES[-1] and pair == 1 and n == 1,
-                )
+            return [
+                (prod[:, n, :], plane == PLANES[0] and pair == 0 and n == 0, plane == PLANES[-1] and pair == 1 and n == 1)
+                for n in range(2)
+            ]
 
         def store(ib, q, o_ps):
             o_sb = rows.tile([P, TB_PER_BANK, P], F32, name="o_sb")
@@ -380,12 +379,19 @@ def tile_kanlayer_t_kernel(tc, x, base_weight, spline_weight, grid, grad_out, ou
                     clamp(after[0], after[1])
                 made[q] = square(ib, c, pair)
 
+        def finish(parts, ib, ch, bank):
+            for part, first, last in parts:
+                add_up(part, bank, first, last)
+            if parts[-1][2]:
+                store(ib, ch, bank)
+
         with tc.manual_schedule():
             clamp(0, 0)
             for q in range(AHEAD):
                 square_ahead(q)
             sums = [mx_sum(0, PLANES[0], ch) for ch in range(N_CHUNK)]
             banks = [None] * N_CHUNK
+            behind = []
             for r in range(len(jobs) + 1):
                 square_ahead(r + AHEAD)
                 if r < len(jobs):
@@ -404,8 +410,11 @@ def tile_kanlayer_t_kernel(tc, x, base_weight, spline_weight, grid, grad_out, ou
                         ib, plane, pair = jobs[q]
                         if plane == PLANES[0] and pair == 0:
                             banks[ch] = psum_t.tile([P, TB_PER_BANK, P], F32, name="o_ps", tag="bank")
-                        term(ib, plane, pair, made.get(q), sums[ch], ch, banks[ch])
+                        behind.append((term(ib, plane, pair, made.get(q), sums[ch], ch), ib, ch, banks[ch]))
                         if q + 1 < len(jobs) and jobs[q + 1][1] != plane:
                             sums[ch] = mx_sum(jobs[q + 1][0], jobs[q + 1][1], ch)
-                        if plane == PLANES[-1] and pair == 1:
-                            store(ib, ch, banks[ch])
+                        if len(behind) > LAG:
+                            finish(behind[0][0], behind[0][1], behind[0][2], behind[0][3])
+                            behind.remove(behind[0])
+            for parts, ib, ch, bank in behind:
+                finish(parts, ib, ch, bank)

@@ -230,6 +230,9 @@ def tile_kanlayer_t_kernel(tc, x, base_weight, spline_weight, grid, grad_out, ou
         with tc.tile_pool(name="load", bufs=1) as load, tc.tile_pool(name="stream", bufs=2) as stream:
             kn_bf = load.tile([P, N_IB, N_KNOTS], BF16, name="kn_bf")
             nc.sync.dma_start(out=kn_bf[:], in_=grid.rearrange("(n p) k -> p n k", p=P))
+            b_raw = load.tile([P, PACK, IN], BF16, name="b_raw")
+            w_load(0)
+            nc.sync.dma_start(out=b_raw[:], in_=base_weight.rearrange("(p j) i -> p j i", j=PACK))
             x_blocks = x.rearrange("(l t p) i -> l p t i", t=LOAD_TB, p=P)
             g_blocks = grad_out.rearrange("(l t p) o -> l p t o", t=LOAD_TB, p=P)
             x_sbs = []
@@ -242,9 +245,6 @@ def tile_kanlayer_t_kernel(tc, x, base_weight, spline_weight, grid, grad_out, ou
                 g_sb = load.tile([P, LOAD_TB, OUT], BF16, name="g_sb%d" % l)
                 nc.sync.dma_start(out=g_sb[:], in_=g_blocks[l])
                 g_sbs.append(g_sb)
-            b_raw = load.tile([P, PACK, IN], BF16, name="b_raw")
-            w_load(0)
-            nc.sync.dma_start(out=b_raw[:], in_=base_weight.rearrange("(p j) i -> p j i", j=PACK))
             w_load(1)
 
             with tc.manual_schedule():
@@ -271,7 +271,7 @@ def tile_kanlayer_t_kernel(tc, x, base_weight, spline_weight, grid, grad_out, ou
                     for t in range(2):
                         for u in range(2):
                             nc.tensor.transpose(gt_ps[:, t, u, :], g_words[:, 2 * pair + t, u, :], ident_f[:])
-                    nc.scalar.copy(
+                    nc.vector.tensor_copy(
                         out=grp_words[:, pair * 2 * P : (pair + 1) * 2 * P, :].rearrange("p (t k) u -> p t k u", t=2),
                         in_=gt_ps[:].rearrange("p t u k -> p t k u"),
                     )

from contextlib import ExitStack

import concourse.mybir as mybir
from concourse.masks import make_identity

F32 = mybir.dt.float32
BF16 = mybir.dt.bfloat16
U32 = mybir.dt.uint32
U8 = mybir.dt.uint8
E4M3X4 = mybir.dt.float8_e4m3fn_x4
E5M2X4 = mybir.dt.float8_e5m2_x4
ALU = mybir.AluOpType
ACT = mybir.ActivationFunctionType

P = 128
PACK = 4
B = 2048
IN = 512
OUT = 512
N_C = 8
N_KNOTS = 12
N_PIECE = 4
EPS = 1e-8
N_IB = IN // P
N_TB = B // P
CHUNK = 512
N_CHUNK = B // CHUNK
TB_PER_BANK = CHUNK // P
UPWARD = (0, 2)
LOAD_TB = 4
BASE = N_C
PLANES = (0, 1, 2, 3, BASE, 4, 5, 6, 7)
COPY_OF = ("a", "a", "b", "b")
PAIRS = ((0, 2), (1, 3))
AHEAD = 2
LAG = 2

FLOPS = 2 * B * OUT * IN * (N_C + 1)

PATHS = (
    (0, 0, 0, 0, (0, 0, 0)),
    (1, 0, 0, 1, (0, 0, 2)),
    (1, 0, 1, 1, (0, 3, 1)),
    (1, 1, 1, 1, (4, 1, 1)),
    (2, 0, 1, 2, (0, 3, 3)),
    (2, 1, 1, 2, (4, 1, 3)),
    (2, 1, 2, 2, (4, 4, 2)),
    (3, 1, 2, 3, (4, 4, 4)),
)


def spline_tables(nc, tabs, kn_bf):
    vec = nc.vector

    def stack(n, name):
        return tabs.tile([P, n, N_IB, N_C], F32, name=name)

    def per_knot(name):
        return tabs.tile([P, N_IB, N_KNOTS], F32, name=name)

    def spread(ap, n):
        return ap.to_broadcast([P, n, N_IB, N_C])

    shift_at = tabs.tile([P, N_PIECE - 1, N_IB, N_KNOTS], F32, name="shift_at")
    vec.memset(shift_at[:], 0.0)

    tau = stack(5, "tau")
    for e in range(5):
        vec.tensor_copy(out=tau[:, e], in_=kn_bf[:, :, e : e + N_C])
    span = stack(9, "span")
    inv = stack(9, "inv")
    at = {1: 0, 2: 4, 3: 7}
    for s in (3, 2, 1):
        vec.scalar_tensor_tensor(
            out=span[:, at[s] : at[s] + 5 - s], in0=tau[:, s:5], scalar=EPS, in1=tau[:, 0 : 5 - s],
            op0=ALU.add, op1=ALU.subtract,
        )
    rel = stack(5, "rel")
    vec.tensor_sub(out=rel[:], in0=tau[:], in1=spread(tau[:, 2:3], 5))
    kn = per_knot("kn")
    vec.tensor_copy(out=kn[:], in_=kn_bf[:])
    vec.reciprocal(out=inv[:], in_=span[:])

    ends = rel[:, 0:5:4]
    sum13 = stack(1, "sum13")
    prod13 = stack(1, "prod13")
    squared = stack(5, "squared")
    twice = stack(2, "twice")
    sym = tabs.tile([P, 2, len(PATHS), N_IB, N_C], F32, name="sym")
    vec.tensor_add(out=sum13[:, 0], in0=rel[:, 1], in1=rel[:, 3])
    vec.tensor_mul(out=squared[:], in0=rel[:], in1=rel[:])
    vec.tensor_mul(out=prod13[:, 0], in0=rel[:, 1], in1=rel[:, 3])
    pair = stack(4, "pair")
    vec.scalar_tensor_tensor(
        out=pair[:, 0:2], in0=inv[:, 4:6], scalar=3.0, in1=spread(inv[:, 7:8], 2), op0=ALU.mult, op1=ALU.mult
    )
    vec.scalar_tensor_tensor(
        out=pair[:, 2:4], in0=inv[:, 5:7], scalar=3.0, in1=spread(inv[:, 8:9], 2), op0=ALU.mult, op1=ALU.mult
    )
    vec.tensor_scalar_mul(out=sym[:, 0, 0:8:7], in0=ends, scalar1=3.0)
    vec.tensor_scalar_mul(out=sym[:, 0, 1:7:5], in0=ends, scalar1=2.0)
    vec.tensor_add(out=sym[:, 0, 2:6:3], in0=ends, in1=spread(sum13[:], 2))
    vec.scalar_tensor_tensor(out=sym[:, 0, 3], in0=rel[:, 1], scalar=2.0, in1=rel[:, 4], op0=ALU.mult, op1=ALU.add)
    vec.scalar_tensor_tensor(out=sym[:, 0, 4], in0=rel[:, 3], scalar=2.0, in1=rel[:, 0], op0=ALU.mult, op1=ALU.add)
    poly = tabs.tile([P, 3, len(PATHS), N_IB, N_C], F32, name="poly")
    vec.tensor_mul(out=poly[:, 0, 0], in0=pair[:, 0], in1=inv[:, 0])
    vec.scalar_tensor_tensor(
        out=poly[:, 0, 1:4], in0=pair[:, 0:3], scalar=-1.0, in1=spread(inv[:, 1:2], 3), op0=ALU.mult, op1=ALU.mult
    )
    vec.tensor_mul(out=poly[:, 0, 4:7], in0=pair[:, 1:4], in1=spread(inv[:, 2:3], 3))
    vec.scalar_tensor_tensor(out=poly[:, 0, 7], in0=pair[:, 3], scalar=-1.0, in1=inv[:, 3], op0=ALU.mult, op1=ALU.mult)
    vec.scalar_tensor_tensor(out=twice[:, 0], in0=rel[:, 4], scalar=2.0, in1=rel[:, 1], op0=ALU.mult, op1=ALU.add)
    vec.scalar_tensor_tensor(out=twice[:, 1], in0=rel[:, 0], scalar=2.0, in1=rel[:, 3], op0=ALU.mult, op1=ALU.add)
    vec.tensor_scalar_mul(out=sym[:, 1, 0:8:7], in0=squared[:, 0:5:4], scalar1=3.0)
    vec.tensor_copy(out=sym[:, 1, 1:7:5], in_=squared[:, 0:5:4])
    vec.tensor_mul(out=sym[:, 1, 2:6:3], in0=ends, in1=spread(sum13[:], 2))
    vec.tensor_mul(out=sym[:, 1, 3:5], in0=twice[:], in1=rel[:, 1:4:2])
    vec.scalar_tensor_tensor(out=poly[:, 1], in0=poly[:, 0], scalar=-2.0 / 3.0, in1=sym[:, 0], op0=ALU.mult, op1=ALU.mult)
    vec.tensor_add(out=sym[:, 1, 2:6:3], in0=sym[:, 1, 2:6:3], in1=spread(prod13[:], 2))
    vec.scalar_tensor_tensor(out=poly[:, 2], in0=poly[:, 0], scalar=1.0 / 3.0, in1=sym[:, 1], op0=ALU.mult, op1=ALU.mult)

    quad = tabs.tile([P, 3, N_PIECE, N_IB, N_C], F32, name="quad")
    vec.tensor_copy(out=quad[:, :, 0:4:3], in_=poly[:, :, 0:8:7])
    vec.tensor_add(out=quad[:, :, 1:3], in0=poly[:, :, 1:5:3], in1=poly[:, :, 2:6:3])
    vec.tensor_add(out=quad[:, :, 1:3], in0=quad[:, :, 1:3], in1=poly[:, :, 3:7:3])
    gain, lin = quad[:, 0], quad[:, 1]

    size = stack(N_PIECE, "size")
    root = stack(N_PIECE, "root")
    vec.scalar_tensor_tensor(out=size[:], in0=gain, scalar=-1.0, in1=gain, op0=ALU.mult, op1=ALU.max)
    nc.scalar.sqrt(out=root[:], in_=size[:])

    knots = rel[:, 1:4]
    step = tabs.tile([P, 3, N_PIECE - 1, N_IB, N_C], F32, name="step")
    jump = stack(3, "jump")
    steep = stack(3, "steep")
    inv_gain = stack(N_PIECE, "inv_gain")
    bias = stack(N_PIECE, "bias")
    vec.tensor_sub(out=step[:], in0=quad[:, :, 1:4], in1=quad[:, :, 0:3])
    vec.tensor_mul(out=steep[:], in0=gain[:, 1:4], in1=knots)
    vec.reciprocal(out=inv_gain[:], in_=gain)
    vec.tensor_mul(out=jump[:], in0=step[:, 0], in1=knots)
    vec.scalar_tensor_tensor(out=steep[:], in0=steep[:], scalar=2.0, in1=lin[:, 1:4], op0=ALU.mult, op1=ALU.add)
    vec.scalar_tensor_tensor(out=bias[:], in0=lin, scalar=0.5, in1=inv_gain[:], op0=ALU.mult, op1=ALU.mult)
    vec.tensor_add(out=jump[:], in0=jump[:], in1=step[:, 1])
    vec.reciprocal(out=steep[:], in_=steep[:])
    vec.tensor_sub(out=bias[:], in0=bias[:], in1=spread(tau[:, 2:3], N_PIECE))
    vec.tensor_mul(out=jump[:], in0=jump[:], in1=knots)
    vec.tensor_add(out=jump[:], in0=jump[:], in1=step[:, 2])
    vec.tensor_mul(out=jump[:], in0=jump[:], in1=steep[:])

    diff = per_knot("diff")
    room = per_knot("room")
    low = {"a": per_knot("low_a"), "b": per_knot("low_b")}
    high = {"a": per_knot("high_a"), "b": per_knot("high_b")}
    for d in range(1, N_PIECE):
        vec.tensor_copy(out=shift_at[:, d - 1, :, d : d + N_C], in_=jump[:, d - 1])
    vec.tensor_scalar(out=room[:], in0=shift_at[:, 0], scalar1=-1.0, scalar2=0.0, op0=ALU.mult, op1=ALU.max)
    vec.tensor_sub(out=diff[:], in0=shift_at[:, 2], in1=shift_at[:, 1])
    vec.scalar_tensor_tensor(out=room[:], in0=shift_at[:, 1], scalar=-1.0, in1=room[:], op0=ALU.mult, op1=ALU.max)
    vec.tensor_max(out=room[:], in0=room[:], in1=diff[:])
    vec.tensor_sub(out=high["a"][:], in0=kn[:], in1=room[:])
    vec.tensor_sub(out=low["a"][:], in0=high["a"][:], in1=shift_at[:, 0])
    vec.tensor_sub(out=low["b"][:], in0=high["a"][:], in1=shift_at[:, 1])
    vec.tensor_add(out=high["b"][:], in0=high["a"][:], in1=diff[:])

    ratio = stack(N_PIECE, "ratio")
    root_bias = stack(N_PIECE, "root_bias")
    vec.reciprocal(out=ratio[:], in_=root[:])
    lo = stack(N_PIECE, "lo")
    for d in range(N_PIECE):
        vec.tensor_copy(out=lo[:, d], in_=low[COPY_OF[d]][:, :, d : d + N_C])
    vec.tensor_mul(out=ratio[:], in0=ratio[:], in1=size[:])
    vec.tensor_add(out=lo[:], in0=lo[:], in1=bias[:])
    vec.tensor_add(out=root[:], in0=root[:], in1=ratio[:])
    vec.tensor_mul(out=lo[:], in0=lo[:], in1=lo[:])
    vec.tensor_scalar_mul(out=root[:], in0=root[:], scalar1=0.5)
    offset = stack(1, "offset")
    vec.scalar_tensor_tensor(out=lo[:], in0=lo[:], scalar=-1.0, in1=gain, op0=ALU.mult, op1=ALU.mult)
    vec.tensor_mul(out=root_bias[:], in0=root[:], in1=bias[:])
    vec.tensor_add(out=offset[:, 0], in0=lo[:, 1], in1=lo[:, 2])
    vec.tensor_add(out=offset[:, 0], in0=offset[:, 0], in1=lo[:, 3])
    vec.tensor_scalar_mul(out=offset[:, 0], in0=offset[:, 0], scalar1=0.5)
    return low, high, offset, root, root_bias


def tile_kanlayer_t_kernel(tc, x, base_weight, spline_weight, grid, grad_out, out):
    nc = tc.nc
    with ExitStack() as ctx:
        keep = ctx.enter_context(tc.tile_pool(name="keep", bufs=1))
        tabs = ctx.enter_context(tc.tile_pool(name="tabs", bufs=1))
        w_stage = ctx.enter_context(tc.tile_pool(name="w_stage", bufs=1))
        psum_c = ctx.enter_context(tc.psum_pool(name="psum_c", bufs=1))
        psum_t = ctx.enter_context(tc.psum_pool(name="psum_t", bufs=4))

        ident_bf = keep.tile([P, P], BF16, name="ident_bf")
        make_identity(nc, ident_bf[:])
        ident_f = keep.tile([P, P], F32, name="ident_f")
        make_identity(nc, ident_f[:])

        x_t = keep.tile([P, N_IB, B], BF16, name="x_t")
        w_codes = keep.tile([P, N_IB, N_C * P], U32, name="w_codes", align_bytes=64)
        w_scales = keep.tile([P, N_IB, N_C * P], U8, name="w_scales", align_bytes=64)
        b_codes = keep.tile([P, IN], U32, name="b_codes", align_bytes=64)
        b_scales = keep.tile([P, IN], U8, name="b_scales", align_bytes=64)
        g_codes = keep.tile([P, B], U32, name="g_codes", align_bytes=64)
        g_scales = keep.tile([P, B], U8, name="g_scales", align_bytes=64)

        w_raws = [w_stage.tile([P, PACK, P * N_C], BF16, name="w_raw%d" % n) for n in range(2)]
        w_grp = w_stage.tile([P, N_C, P, PACK], BF16, name="w_grp", align_bytes=64)
        w_rows = spline_weight.rearrange("(p j) i c -> p j i c", j=PACK)
        clamped = ctx.enter_context(tc.tile_pool(name="clamped", bufs=4))
        squares = ctx.enter_context(tc.tile_pool(name="squares", bufs=4))

        def w_load(ib):
            nc.sync.dma_start(
                out=w_raws[ib % 2][:].rearrange("p j (i c) -> p j i c", c=N_C), in_=w_rows[:, :, ib * P : (ib + 1) * P, :]
            )

        def w_view(ib):
            return w_raws[ib % 2][:].rearrange("p j (i c) -> p c i j", c=N_C)

        def w_quantize(ib):
            nc.vector.quantize_mx(
                out=w_codes[:, ib, :].bitcast(E4M3X4),
                scales=w_scales[:, ib, :],
                in_=w_grp[:].rearrange("p c i j -> p (c i j)"),
            )

        with tc.tile_pool(name="load", bufs=1) as load, tc.tile_pool(name="stream", bufs=2) as stream:
            kn_bf = load.tile([P, N_IB, N_KNOTS], BF16, name="kn_bf")
            nc.sync.dma_start(out=kn_bf[:], in_=grid.rearrange("(n p) k -> p n k", p=P))
            b_raw = load.tile([P, PACK, IN], BF16, name="b_raw")
            w_load(0)
            nc.sync.dma_start(out=b_raw[:], in_=base_weight.rearrange("(p j) i -> p j i", j=PACK))
            x_blocks = x.rearrange("(l t p) i -> l p t i", t=LOAD_TB, p=P)
            g_blocks = grad_out.rearrange("(l t p) o -> l p t o", t=LOAD_TB, p=P)
            x_sbs = []
            for l in range(N_TB // LOAD_TB):
                x_sb = load.tile([P, LOAD_TB, IN], BF16, name="x_sb%d" % l)
                nc.sync.dma_start(out=x_sb[:], in_=x_blocks[l])
                x_sbs.append(x_sb)
            g_sbs = []
            for l in range(N_TB // LOAD_TB):
                g_sb = load.tile([P, LOAD_TB, OUT], BF16, name="g_sb%d" % l)
                nc.sync.dma_start(out=g_sb[:], in_=g_blocks[l])
                g_sbs.append(g_sb)
            w_load(1)

            with tc.manual_schedule():
                low, high, offset, root, root_bias = spline_tables(nc, tabs, kn_bf)

            for ib in range(N_IB):
                for half in range(2):
                    xt_ps = psum_t.tile([P, 8, P], BF16, name="xt_ps", tag="bank")
                    for t in range(8):
                        tb = half * 8 + t
                        nc.tensor.transpose(
                            xt_ps[:, t, :], x_sbs[tb // LOAD_TB][:, tb % LOAD_TB, ib * P : (ib + 1) * P], ident_bf[:]
                        )
                    nc.scalar.copy(
                        out=x_t[:, ib, half * 8 * P : (half + 1) * 8 * P], in_=xt_ps[:].rearrange("p t k -> p (t k)")
                    )

            for l in range(N_TB // LOAD_TB):
                g_words = g_sbs[l][:].bitcast(F32).rearrange("p t (w u) -> p t u w", u=2)
                g_grp = stream.tile([P, LOAD_TB * P, PACK], BF16, name="g_grp", align_bytes=64)
                grp_words = g_grp[:].bitcast(F32)
                for pair in range(LOAD_TB // 2):
                    gt_ps = psum_t.tile([P, 2, 2, P], F32, name="gt_ps", tag="bank")
                    for t in range(2):
                        for u in range(2):
                            nc.tensor.transpose(gt_ps[:, t, u, :], g_words[:, 2 * pair + t, u, :], ident_f[:])
                    nc.vector.tensor_copy(
                        out=grp_words[:, pair * 2 * P : (pair + 1) * 2 * P, :].rearrange("p (t k) u -> p t k u", t=2),
                        in_=gt_ps[:].rearrange("p t u k -> p t k u"),
                    )
                toks = slice(l * LOAD_TB * P, (l + 1) * LOAD_TB * P)
                nc.vector.quantize_mx(
                    out=g_codes[:, toks].bitcast(E5M2X4),
                    scales=g_scales[:, toks],
                    in_=g_grp[:].rearrange("p k t -> p (k t)"),
                )

            nc.scalar.copy(out=w_grp[:], in_=w_view(0))
            w_quantize(0)
            b_grp = load.tile([P, IN, PACK], BF16, name="b_grp", align_bytes=64)
            nc.scalar.copy(out=b_grp[:], in_=b_raw[:].rearrange("p j i -> p i j"))
            nc.vector.quantize_mx(
                out=b_codes[:].bitcast(E4M3X4), scales=b_scales[:], in_=b_grp[:].rearrange("p i j -> p (i j)")
            )

        prods = ctx.enter_context(tc.tile_pool(name="prods", bufs=8))
        rows = ctx.enter_context(tc.tile_pool(name="rows", bufs=3))
        out_rows = out.rearrange("(q t p) f -> q p t f", t=TB_PER_BANK, p=P)
        chunks = [slice(ch * CHUNK, (ch + 1) * CHUNK) for ch in range(N_CHUNK)]
        copies = {}

        def clamp(ib, c):
            for d in range(N_PIECE):
                k = c + d
                if (ib, k, COPY_OF[d]) not in copies:
                    u = clamped.tile([P, B], BF16, name="u_" + COPY_OF[d])
                    nc.gpsimd.tensor_scalar(
                        out=u[:], in0=x_t[:, ib, :],
                        scalar1=high[COPY_OF[d]][:, ib, k + 1 : k + 2], scalar2=low[COPY_OF[d]][:, ib, k : k + 1],
                        op0=ALU.min, op1=ALU.max,
                    )
                    copies[(ib, k, COPY_OF[d])] = u

        def square(ib, c, pair):
            one = slice(c, c + 1)
            s = squares.tile([P, 2, B], F32, name="sq")
            for n, d in enumerate(PAIRS[pair]):
                nc.scalar.activation(
                    out=s[:, n, :], in_=copies[(ib, c + d, COPY_OF[d])][:], func=ACT.Square,
                    bias=root_bias[:, d, ib, one], scale=root[:, d, ib, one],
                )
            return s

        def mx_sum(ib, plane, ch):
            c_ps = psum_c.tile([P, CHUNK], F32, name="c_ps%d" % ch)
            if plane == BASE:
                codes, scales = b_codes[:, ib * P : (ib + 1) * P], b_scales[:, ib * P : (ib + 1) * P]
            else:
                codes, scales = w_codes[:, ib, plane * P : (plane + 1) * P], w_scales[:, ib, plane * P : (plane + 1) * P]
            nc.tensor.matmul_mx(
                out=c_ps[:],
                lhsT=codes.bitcast(E4M3X4),
                lhsT_scale=scales,
                rhs=g_codes[:, chunks[ch]].bitcast(E5M2X4),
                rhs_scale=g_scales[:, chunks[ch]],
                start=True,
                stop=True,
            )
            return c_ps

        def add_up(prod, bank, first, last):
            for t in range(TB_PER_BANK):
                nc.tensor.matmul(
                    bank[:, t, :], lhsT=prod[:, t * P : (t + 1) * P], rhs=ident_f[:], is_transpose=True,
                    start=(first and t == 0), stop=(last and t == TB_PER_BANK - 1),
                )

        def term(ib, plane, pair, s, c_ps, ch):
            if plane == BASE:
                prod = prods.tile([P, 2, CHUNK], F32, name="prod")
                nc.vector.tensor_copy(out=prod[:, 0, :], in_=c_ps[:])
                return [(prod[:, 0, :], False, False)]
            prod = prods.tile([P, 2, CHUNK], F32, name="prod")
            twice = c_ps[:].unsqueeze(1).to_broadcast([P, 2, CHUNK])
            if pair == 0:
                nc.vector.scalar_tensor_tensor(
                    out=prod[:], in0=s[:, :, chunks[ch]], scalar=offset[:, 0, ib, plane : plane + 1], in1=twice,
                    op0=ALU.add, op1=ALU.mult,
                )
            else:
                nc.vector.scalar_tensor_tensor(
                    out=prod[:], in0=s[:, :, chunks[ch]], scalar=-1.0, in1=twice, op0=ALU.mult, op1=ALU.mult
                )
            return [
                (prod[:, n, :], plane == PLANES[0] and pair == 0 and n == 0, plane == PLANES[-1] and pair == 1 and n == 1)
                for n in range(2)
            ]

        def store(ib, q, o_ps):
            o_sb = rows.tile([P, TB_PER_BANK, P], F32, name="o_sb")
            nc.scalar.copy(out=o_sb[:], in_=o_ps[:])
            nc.sync.dma_start(out=out_rows[q][:, :, ib * P : (ib + 1) * P], in_=o_sb[:])

        jobs = [(ib, plane, pair) for ib in range(N_IB) for plane in PLANES for pair in range(1 if plane == BASE else 2)]
        made = {}

        def square_ahead(q):
            if q < len(jobs) and jobs[q][1] != BASE:
                ib, c, pair = jobs[q]
                after = (ib, c + 1) if c + 1 < N_C else (ib + 1, 0)
                if pair == 0 and after[0] < N_IB:
                    clamp(after[0], after[1])
                made[q] = square(ib, c, pair)

        def finish(parts, ib, ch, bank):
            for part, first, last in parts:
                add_up(part, bank, first, last)
            if parts[-1][2]:
                store(ib, ch, bank)

        with tc.manual_schedule():
            clamp(0, 0)
            for q in range(AHEAD):
                square_ahead(q)
            sums = [mx_sum(0, PLANES[0], ch) for ch in range(N_CHUNK)]
            banks = [None] * N_CHUNK
            behind = []
            for r in range(len(jobs) + 1):
                square_ahead(r + AHEAD)
                if r < len(jobs):
                    ib, plane, pair = jobs[r]
                    if pair == 0 and plane == PLANES[1] and ib + 1 < N_IB:
                        nc.gpsimd.tensor_scalar(
                            out=w_grp[:], in0=w_view(ib + 1), scalar1=1.0, scalar2=0.0, op0=ALU.mult, op1=ALU.add
                        )
                    if pair == 0 and plane == PLANES[2] and ib + 2 < N_IB:
                        w_load(ib + 2)
                    if pair == 0 and plane == PLANES[5] and ib + 1 < N_IB:
                        w_quantize(ib + 1)
                for ch in range(N_CHUNK):
                    q = r - ch // 2
                    if 0 <= q < len(jobs):
                        ib, plane, pair = jobs[q]
                        if plane == PLANES[0] and pair == 0:
                            banks[ch] = psum_t.tile([P, TB_PER_BANK, P], F32, name="o_ps", tag="bank")
                        behind.append((term(ib, plane, pair, made.get(q), sums[ch], ch), ib, ch, banks[ch]))
                        if q + 1 < len(jobs) and jobs[q + 1][1] != plane:
                            sums[ch] = mx_sum(jobs[q + 1][0], jobs[q + 1][1], ch)
                        if len(behind) > LAG:
                            finish(behind[0][0], behind[0][1], behind[0][2], behind[0][3])
                            behind.remove(behind[0])
            for parts, ib, ch, bank in behind:
                finish(parts, ib, ch, bank)
